import numpy as np
import ml_dtypes


def mxq(x, axis, fmt="e4m3"):
    dtype, down = {"e4m3": (ml_dtypes.float8_e4m3fn, 7), "e5m2": (ml_dtypes.float8_e5m2, 14)}[fmt]
    v = np.moveaxis(np.asarray(x, np.float32).astype(ml_dtypes.bfloat16).astype(np.float64), axis, -1)
    blocks = v.reshape(v.shape[:-1] + (-1, 32))
    amax = np.abs(blocks).max(-1, keepdims=True)
    byte = np.maximum(np.where(amax > 0, np.frexp(amax)[1] - 1 + 127, 0) - down, 1)
    scale = np.exp2(byte - 127.0)
    codes = (blocks / scale).astype(np.float32).astype(dtype).astype(np.float64)
    return np.moveaxis((codes * scale).reshape(v.shape), -1, axis)


WIDE = False


def mx_kscale(k):
    if not WIDE:
        return np.ones(k)
    levels = np.array([10, -10, 5, -5, 0])
    if k % 512:
        return np.exp2(np.random.permutation(np.resize(levels, k // 32))).repeat(32)
    a = np.empty((k // 512, 16))
    for p in range(k // 512):
        a[p, :8] = np.random.permutation(np.resize(levels, 8))
        for g in range(8):
            far = levels[np.abs(levels - a[p, g]) >= 10]
            a[p, g + 8] = far[np.random.randint(len(far))]
    return np.exp2(a.ravel()).repeat(32)


BF16 = ml_dtypes.bfloat16


def bf(x):
    return np.asarray(x, np.float32).astype(BF16)


def f64(x):
    return np.asarray(x).astype(np.float64)


B, T, C, KW = 2, 1024, 512, 3
PAD = KW // 2


def draw0():
    s = mx_kscale(C)
    return {"x": bf(np.random.standard_normal((B, T, C)) * s),
            "w1": bf(np.random.standard_normal((C, C)) / np.sqrt(C) / s[None, :]),
            "b1": bf(np.random.standard_normal(C) * 0.2),
            "w2": bf(np.random.standard_normal((C, KW)) * 0.8),
            "b2": bf(np.random.standard_normal(C) * 0.2)}


def core(x, w1, b1, w2, b2):
    h = (mxq(f64(x), 2, "e4m3") @ mxq(f64(w1), 1, "e4m3").T) + f64(b1)
    hp = np.pad(h, ((0, 0), (PAD, PAD), (0, 0)))
    taps = f64(w2)
    y = hp[:, 0:T, :] * taps[:, 0]
    for j in range(1, KW):
        y = y + hp[:, j:j + T, :] * taps[:, j]
    return y + f64(b2)


def e4m3fn_bytes(y):
    return np.clip(np.asarray(y, np.float64), -448.0, 448.0).astype(np.float32).astype(ml_dtypes.float8_e4m3fn).view(np.uint8)


def e4m3fn_values(b):
    return np.asarray(b, np.uint8).view(ml_dtypes.float8_e4m3fn).astype(np.float64)


def setup_inputs():
    d = draw0()
    x0 = np.asarray(d['x']).astype(np.float64)
    s = (np.max(np.abs(x0), axis=(0, 1), keepdims=True) / 448.0).astype(np.float32)
    out = {}
    for k, v in d.items():
        if k == 'x':
            out['x_bytes'] = e4m3fn_bytes(x0 / s.astype(np.float64))
            out['x_scale'] = s
        else:
            out[k] = v
    return out


def reference(x_bytes, x_scale, w1, b1, w2, b2):
    return core(e4m3fn_values(x_bytes) * x_scale.astype(np.float64), w1, b1, w2, b2)

@@ -1,0 +1,246 @@
+from contextlib import ExitStack
+
+import concourse.masks as masks
+import concourse.mybir as mybir
+
+F32 = mybir.dt.float32
+BF16 = mybir.dt.bfloat16
+U32 = mybir.dt.uint32
+U8 = mybir.dt.uint8
+FP8 = mybir.dt.float8_e4m3fn
+FP8X4 = mybir.dt.float8_e4m3fn_x4
+ALU = mybir.AluOpType
+ACT = mybir.ActivationFunctionType
+
+NB, T, C, D = 2, 1024, 512, 512
+P = 128
+CHUNK = 512
+NCH = NB * T // CHUNK
+MT = D // P
+PADY = 16
+
+FLOPS = 2 * NB * T * C * D + 6 * NB * T * D
+
+
+CAST = ("ss", "ss", "ss", "ss")
+BETA = ((2, 3), (3,))
+
+
+def tile_cvim_pa_kernel(tc, x_bytes, x_scale, w1, b1, w2, b2, out):
+    nc = tc.nc
+    xflat = x_bytes.rearrange("b t k -> (b t) k")
+    oflat = out.rearrange("b t d -> (b t) d")
+
+    with ExitStack() as ctx:
+        const = ctx.enter_context(tc.tile_pool(name="const", bufs=1))
+        rows = ctx.enter_context(tc.tile_pool(name="rows", bufs=1))
+        outp = ctx.enter_context(tc.tile_pool(name="outp", bufs=16))
+        psh = ctx.enter_context(tc.psum_pool(name="psh", bufs=1))
+        pst = ctx.enter_context(tc.psum_pool(name="pst", bufs=4))
+
+        s_kp = const.tile([P, 4], F32, name="s_kp")
+        nc.sync.dma_start(out=s_kp[:], in_=x_scale.rearrange("a b (p t) -> (a b p) t", t=4))
+        xb = []
+        for c in range(NCH):
+            xbt = const.tile([P, 4, C], U8, name="xbytes%d" % c)
+            xb.append(xbt)
+        for hf in range(2):
+            nc.sync.dma_start(out=xb[0][:, 2 * hf:2 * hf + 2, :], in_=xflat[hf * 2 * P:(hf + 1) * 2 * P, :].rearrange("(i p) k -> p i k", p=P))
+        w_sb = const.tile([P, MT, C], BF16, name="w_sb")
+        nc.sync.dma_start(out=w_sb[:], in_=w1.rearrange("(p m) k -> p m k", m=MT))
+        for c in range(1, NCH):
+            nc.sync.dma_start(out=xb[c][:], in_=xflat[c * CHUNK:(c + 1) * CHUNK, :].rearrange("(i p) k -> p i k", p=P))
+        a_bf = const.tile([P, MT, 3], BF16, name="a_bf")
+        nc.scalar.dma_start(out=a_bf[:], in_=w2.rearrange("(p m) j -> p m j", m=MT))
+        b1_bf = const.tile([P, MT], BF16, name="b1_bf")
+        nc.scalar.dma_start(out=b1_bf[:], in_=b1.rearrange("(p m) -> p m", m=MT))
+        b2_bf = const.tile([P, MT], BF16, name="b2_bf")
+        nc.scalar.dma_start(out=b2_bf[:], in_=b2.rearrange("(p m) -> p m", m=MT))
+
+        ident = const.tile([P, P], F32, name="ident")
+        masks.make_identity(nc, ident[:])
+        warm = const.tile([P, 2], F32, name="warm")
+        nc.vector.memset(warm[:, 0:1], 0.0)
+        nc.scalar.activation(out=warm[:, 1:2], in_=warm[:, 0:1], func=ACT.Identity)
+
+        a_f = const.tile([P, MT, 3], F32, name="a_f")
+        nc.gpsimd.tensor_copy(out=a_f[:], in_=a_bf[:])
+        b1_f = const.tile([P, MT], F32, name="b1_f")
+        nc.gpsimd.tensor_copy(out=b1_f[:], in_=b1_bf[:])
+        b2_f = const.tile([P, MT], F32, name="b2_f")
+        nc.gpsimd.tensor_copy(out=b2_f[:], in_=b2_bf[:])
+        pad0 = const.tile([P, MT], F32, name="pad0")
+        kall = const.tile([P, MT], F32, name="kall")
+        na2b1 = const.tile([P, MT], F32, name="na2b1")
+        tmp = const.tile([P, MT], F32, name="tmp")
+        nc.gpsimd.tensor_tensor(out=pad0[:], in0=a_f[:, :, 1], in1=a_f[:, :, 2], op=ALU.add)
+        nc.gpsimd.tensor_tensor(out=pad0[:], in0=pad0[:], in1=b1_f[:], op=ALU.mult)
+        nc.gpsimd.tensor_tensor(out=pad0[:], in0=pad0[:], in1=b2_f[:], op=ALU.add)
+        nc.gpsimd.tensor_tensor(out=tmp[:], in0=a_f[:, :, 0], in1=b1_f[:], op=ALU.mult)
+        nc.gpsimd.tensor_tensor(out=kall[:], in0=pad0[:], in1=tmp[:], op=ALU.add)
+        nc.gpsimd.tensor_tensor(out=na2b1[:], in0=a_f[:, :, 2], in1=b1_f[:], op=ALU.mult)
+        nc.gpsimd.tensor_scalar(out=na2b1[:], in0=na2b1[:], scalar1=-1.0, scalar2=0.0, op0=ALU.mult, op1=ALU.add)
+
+        g0row, vrow, yrow = {}, {}, {}
+        for b in range(NB):
+            for m in range(MT):
+                g0t = rows.tile([P, 1 + T], F32, name="g0_%d_%d" % (b, m))
+                vt = rows.tile([P, 1 + T], F32, name="v_%d_%d" % (b, m))
+                yt = rows.tile([P, PADY + T], F32, name="y_%d_%d" % (b, m))
+                g0row[(b, m)] = g0t
+                vrow[(b, m)] = vt
+                yrow[(b, m)] = yt
+                nc.gpsimd.tensor_copy(out=g0t[:, 0:1], in_=pad0[:, m:m + 1])
+                if m in BETA[b]:
+                    nc.gpsimd.tensor_copy(out=yt[:, PADY - 1 + T:PADY + T], in_=na2b1[:, m:m + 1])
+                else:
+                    nc.vector.memset(vt[:, 0:1], 0.0)
+
+        wg = const.tile([P, D, 4], BF16, name="wg", align_bytes=64)
+        wc = const.tile([P, D], U32, name="wc", align_bytes=64)
+        ws = const.tile([P, D], U8, name="ws", align_bytes=64)
+        xw_t, xg_t, xc_t, xs_t, h_t, yT_t, ysb_t = {}, {}, {}, {}, {}, {}, {}
+        for c in range(NCH):
+            xw_t[c] = const.tile([P, 4, C], BF16, name="xw%d" % c)
+            xg_t[c] = const.tile([P, CHUNK, 4], BF16, name="xg%d" % c, align_bytes=64)
+            xc_t[c] = const.tile([P, CHUNK], U32, name="xc%d" % c, align_bytes=64)
+            xs_t[c] = const.tile([P, CHUNK], U8, name="xs%d" % c, align_bytes=64)
+
+        def widen(c):
+            for hf in range(2):
+                dst = xw_t[c][:, 2 * hf:2 * hf + 2, :].rearrange("p i k -> p (i k)")
+                src = xb[c][:, 2 * hf:2 * hf + 2, :].rearrange("p i k -> p (i k)").bitcast(FP8)
+                if CAST[c][hf] == "s":
+                    nc.scalar.copy(out=dst, in_=src)
+                else:
+                    nc.vector.tensor_copy(out=dst, in_=src)
+
+        def turn(src, dst3, pair, scaled=True):
+            xt = pst.tile([P, 2, 2, P], F32, tag="t")
+            for i2 in range(2):
+                words = src[:, 2 * pair + i2, :].bitcast(F32)
+                for u in range(2):
+                    nc.tensor.transpose(xt[:, i2, u, :], words[:, u:C // 2:2], ident[:])
+            if scaled:
+                for i2 in range(2):
+                    n0 = (2 * pair + i2) * P
+                    nc.vector.tensor_tensor(out=dst3[:, n0:n0 + P, :].rearrange("p n (u e) -> p n u e", u=2),
+                                            in0=xt[:, i2, :, :].rearrange("p u r -> p (u r)").bitcast(BF16).rearrange("p (u r e) -> p r u e", u=2, e=2),
+                                            in1=s_kp[:].rearrange("p (u e) -> p u e", u=2).unsqueeze(1).to_broadcast([P, P, 2, 2]), op=ALU.mult)
+            else:
+                dst = dst3[:, 2 * pair * P:(2 * pair + 2) * P, :].rearrange("p n j -> p (n j)").bitcast(F32)
+                nc.scalar.copy(out=dst.rearrange("p (i r u) -> p i r u", i=2, u=2), in_=xt[:].rearrange("p i u r -> p i r u"))
+
+        def quant(c):
+            nc.vector.quantize_mx(out=xc_t[c][:].bitcast(FP8X4), scales=xs_t[c][:], in_=xg_t[c][:].rearrange("p n j -> p (n j)"))
+
+        def mm(c, m):
+            h = psh.tile([P, CHUNK], F32, tag="h%d" % m)
+            h_t[(c, m)] = h
+            nc.tensor.matmul_mx(out=h[:], lhsT=wc[:, m * P:(m + 1) * P].bitcast(FP8X4), lhsT_scale=ws[:, m * P:(m + 1) * P],
+                                rhs=xc_t[c][:].bitcast(FP8X4), rhs_scale=xs_t[c][:], start=True, stop=True)
+
+        def g0(c, m):
+            b, c0 = c // 2, (c % 2) * CHUNK
+            nc.scalar.activation(out=g0row[(b, m)][:, 1 + c0:1 + c0 + CHUNK], in_=h_t[(c, m)][:], func=ACT.Identity,
+                                 scale=a_f[:, m, 0:1], bias=kall[:, m:m + 1])
+            if m in BETA[b]:
+                nc.scalar.activation(out=yrow[(b, m)][:, PADY - 1 + c0:PADY - 1 + c0 + CHUNK], in_=h_t[(c, m)][:], func=ACT.Identity,
+                                     scale=a_f[:, m, 2:3])
+
+        def vv(c, m, lo=0, hi=CHUNK):
+            b, c0 = c // 2, (c % 2) * CHUNK
+            nc.vector.scalar_tensor_tensor(out=vrow[(b, m)][:, 1 + c0 + lo:1 + c0 + hi], in0=h_t[(c, m)][:, lo:hi], scalar=a_f[:, m, 1:2],
+                                           in1=g0row[(b, m)][:, c0 + lo:c0 + hi], op0=ALU.mult, op1=ALU.add)
+
+        def zz(c, m, lo=0, hi=CHUNK):
+            b, c0 = c // 2, (c % 2) * CHUNK
+            if m in BETA[b]:
+                return
+            nc.vector.scalar_tensor_tensor(out=yrow[(b, m)][:, PADY - 1 + c0 + lo:PADY - 1 + c0 + hi], in0=h_t[(c, m)][:, lo:hi], scalar=a_f[:, m, 2:3],
+                                           in1=vrow[(b, m)][:, c0 + lo:c0 + hi], op0=ALU.mult, op1=ALU.add)
+            if c0 + hi == T:
+                nc.vector.tensor_scalar(out=yrow[(b, m)][:, PADY + T - 1:PADY + T], in0=vrow[(b, m)][:, T:T + 1],
+                                        scalar1=na2b1[:, m:m + 1], scalar2=None, op0=ALU.add)
+
+        def ty_m(b, i, m):
+            t0 = i * P
+            if (b, i) not in yT_t:
+                yT_t[(b, i)] = pst.tile([P, MT, P], F32, tag="t", name="yT")
+            yT = yT_t[(b, i)]
+            if m in BETA[b]:
+                nc.tensor.matmul(out=yT[:, m, :], lhsT=vrow[(b, m)][:, 1 + t0:1 + t0 + P], rhs=ident[:], is_transpose=True, start=True, stop=False)
+                nc.tensor.matmul(out=yT[:, m, :], lhsT=yrow[(b, m)][:, PADY + t0:PADY + t0 + P], rhs=ident[:], is_transpose=True, start=False, stop=True)
+            else:
+                nc.tensor.transpose(yT[:, m, :], yrow[(b, m)][:, PADY + t0:PADY + t0 + P], ident[:])
+
+        def ty(b, i):
+            for m in range(MT):
+                ty_m(b, i, m)
+
+        def ey(b, i, eng):
+            t0 = i * P
+            ysb = outp.tile([P, D], F32, tag="ysb")
+            dst, src = ysb[:].rearrange("p (q m) -> p q m", m=MT), yT_t[(b, i)][:].rearrange("p m q -> p q m")
+            if eng == "s":
+                nc.scalar.copy(out=dst, in_=src)
+            else:
+                nc.vector.tensor_copy(out=dst, in_=src)
+            nc.sync.dma_start(out=oflat[b * T + t0:b * T + t0 + P, :], in_=ysb[:])
+
+        def tiles_of(c):
+            return [(c // 2, i) for i in ([0, 1, 2] if c % 2 == 0 else [3, 4, 5, 6, 7])]
+
+        def back(c, engs):
+            for j, (b, i) in enumerate(tiles_of(c)):
+                ty(b, i)
+                ey(b, i, engs[j % len(engs)])
+
+        widen(0)
+        turn(w_sb, wg, 0, False)
+        turn(w_sb, wg, 1, False)
+        turn(xw_t[0], xg_t[0], 0)
+        turn(xw_t[0], xg_t[0], 1)
+        nc.vector.quantize_mx(out=wc[:].bitcast(FP8X4), scales=ws[:], in_=wg[:].rearrange("p n j -> p (n j)"))
+        quant(0)
+        widen(1)
+        mm(0, 0)
+        g0(0, 0)
+        mm(0, 1)
+        g0(0, 1)
+        mm(0, 3)
+        mm(0, 2)
+        turn(xw_t[1], xg_t[1], 0)
+        turn(xw_t[1], xg_t[1], 1)
+        g0(0, 3)
+        g0(0, 2)
+        for c in range(NCH):
+            nxt = c + 1 < NCH
+            vv(c, 0)
+            vv(c, 1)
+            zz(c, 0)
+            if c > 0:
+                back(c - 1, "s")
+            if nxt:
+                quant(c + 1)
+                mm(c + 1, 0)
+                g0(c + 1, 0)
+            if c + 2 < NCH:
+                widen(c + 2)
+                turn(xw_t[c + 2], xg_t[c + 2], 0)
+                turn(xw_t[c + 2], xg_t[c + 2], 1)
+            vv(c, 2)
+            zz(c, 1)
+            if nxt:
+                mm(c + 1, 1)
+                g0(c + 1, 1)
+            vv(c, 3)
+            zz(c, 3)
+            if nxt:
+                mm(c + 1, 3)
+                g0(c + 1, 3)
+            zz(c, 2)
+            if nxt:
+                mm(c + 1, 2)
+                g0(c + 1, 2)
+        back(NCH - 1, "sv")

@@ -22,7 +22,8 @@ PADY = 16
 FLOPS = 2 * NB * T * C * D + 6 * NB * T * D
 
 
-CAST = ("ss", "ss", "ss", "ss")
+CAST = ("bb", "ss", "ss", "ss")
+XROW = ((), ())
 BETA = ((2, 3), (3,))
 
 
@@ -39,7 +40,7 @@ def tile_cvim_pa_kernel(tc, x_bytes, x_scale, w1, b1, w2, b2, out):
         pst = ctx.enter_context(tc.psum_pool(name="pst", bufs=4))
 
         s_kp = const.tile([P, 4], F32, name="s_kp")
-        nc.sync.dma_start(out=s_kp[:], in_=x_scale.rearrange("a b (p t) -> (a b p) t", t=4))
+        nc.scalar.dma_start(out=s_kp[:], in_=x_scale.rearrange("a b (p t) -> (a b p) t", t=4))
         xb = []
         for c in range(NCH):
             xbt = const.tile([P, 4, C], U8, name="xbytes%d" % c)
@@ -81,9 +82,18 @@ def tile_cvim_pa_kernel(tc, x_bytes, x_scale, w1, b1, w2, b2, out):
         nc.gpsimd.tensor_tensor(out=na2b1[:], in0=a_f[:, :, 2], in1=b1_f[:], op=ALU.mult)
         nc.gpsimd.tensor_scalar(out=na2b1[:], in0=na2b1[:], scalar1=-1.0, scalar2=0.0, op0=ALU.mult, op1=ALU.add)
 
-        g0row, vrow, yrow = {}, {}, {}
+        g0row, vrow, yrow, xrow = {}, {}, {}, {}
         for b in range(NB):
             for m in range(MT):
+                if m in XROW[b]:
+                    hst = rows.tile([P, T], F32, name="hs_%d_%d" % (b, m))
+                    p0t = rows.tile([P, 1 + T], F32, name="p0_%d_%d" % (b, m))
+                    p1t = rows.tile([P, T], F32, name="p1_%d_%d" % (b, m))
+                    p2t = rows.tile([P, T + 1], F32, name="p2_%d_%d" % (b, m))
+                    xrow[(b, m)] = (hst, p0t, p1t, p2t)
+                    nc.vector.memset(p0t[:, 0:1], 0.0)
+                    nc.vector.memset(p2t[:, T:T + 1], 0.0)
+                    continue
                 g0t = rows.tile([P, 1 + T], F32, name="g0_%d_%d" % (b, m))
                 vt = rows.tile([P, 1 + T], F32, name="v_%d_%d" % (b, m))
                 yt = rows.tile([P, PADY + T], F32, name="y_%d_%d" % (b, m))
@@ -108,6 +118,10 @@ def tile_cvim_pa_kernel(tc, x_bytes, x_scale, w1, b1, w2, b2, out):
 
         def widen(c):
             for hf in range(2):
+                if CAST[c][hf] == "b":
+                    nc.scalar.copy(out=xw_t[c][:, 2 * hf, :], in_=xb[c][:, 2 * hf, :].bitcast(FP8))
+                    nc.vector.tensor_copy(out=xw_t[c][:, 2 * hf + 1, :], in_=xb[c][:, 2 * hf + 1, :].bitcast(FP8))
+                    continue
                 dst = xw_t[c][:, 2 * hf:2 * hf + 2, :].rearrange("p i k -> p (i k)")
                 src = xb[c][:, 2 * hf:2 * hf + 2, :].rearrange("p i k -> p (i k)").bitcast(FP8)
                 if CAST[c][hf] == "s":
@@ -120,13 +134,12 @@ def tile_cvim_pa_kernel(tc, x_bytes, x_scale, w1, b1, w2, b2, out):
             for i2 in range(2):
                 words = src[:, 2 * pair + i2, :].bitcast(F32)
                 for u in range(2):
-                    nc.tensor.transpose(xt[:, i2, u, :], words[:, u:C // 2:2], ident[:])
+                    nc.tensor.transpose(xt[:, u, i2, :] if scaled else xt[:, i2, u, :], words[:, u:C // 2:2], ident[:])
             if scaled:
-                for i2 in range(2):
-                    n0 = (2 * pair + i2) * P
-                    nc.vector.tensor_tensor(out=dst3[:, n0:n0 + P, :].rearrange("p n (u e) -> p n u e", u=2),
-                                            in0=xt[:, i2, :, :].rearrange("p u r -> p (u r)").bitcast(BF16).rearrange("p (u r e) -> p r u e", u=2, e=2),
-                                            in1=s_kp[:].rearrange("p (u e) -> p u e", u=2).unsqueeze(1).to_broadcast([P, P, 2, 2]), op=ALU.mult)
+                n0 = 2 * pair * P
+                nc.vector.tensor_tensor(out=dst3[:, n0:n0 + 2 * P, :].rearrange("p n (u e) -> p n u e", u=2),
+                                        in0=xt[:].rearrange("p u i r -> p (u i r)").bitcast(BF16).rearrange("p (u n e) -> p n u e", u=2, e=2),
+                                        in1=s_kp[:].rearrange("p (u e) -> p u e", u=2).unsqueeze(1).to_broadcast([P, 2 * P, 2, 2]), op=ALU.mult)
             else:
                 dst = dst3[:, 2 * pair * P:(2 * pair + 2) * P, :].rearrange("p n j -> p (n j)").bitcast(F32)
                 nc.scalar.copy(out=dst.rearrange("p (i r u) -> p i r u", i=2, u=2), in_=xt[:].rearrange("p i u r -> p i r u"))
@@ -142,6 +155,9 @@ def tile_cvim_pa_kernel(tc, x_bytes, x_scale, w1, b1, w2, b2, out):
 
         def g0(c, m):
             b, c0 = c // 2, (c % 2) * CHUNK
+            if m in XROW[b]:
+                nc.scalar.activation(out=xrow[(b, m)][0][:, c0:c0 + CHUNK], in_=h_t[(c, m)][:], func=ACT.Identity, bias=b1_f[:, m:m + 1])
+                return
             nc.scalar.activation(out=g0row[(b, m)][:, 1 + c0:1 + c0 + CHUNK], in_=h_t[(c, m)][:], func=ACT.Identity,
                                  scale=a_f[:, m, 0:1], bias=kall[:, m:m + 1])
             if m in BETA[b]:
@@ -150,12 +166,18 @@ def tile_cvim_pa_kernel(tc, x_bytes, x_scale, w1, b1, w2, b2, out):
 
         def vv(c, m, lo=0, hi=CHUNK):
             b, c0 = c // 2, (c % 2) * CHUNK
+            if m in XROW[b]:
+                hst, p0t, p1t, p2t = xrow[(b, m)]
+                nc.vector.tensor_scalar(out=p0t[:, 1 + c0:1 + c0 + CHUNK], in0=hst[:, c0:c0 + CHUNK], scalar1=a_f[:, m, 0:1], scalar2=None, op0=ALU.mult)
+                nc.vector.tensor_scalar(out=p1t[:, c0:c0 + CHUNK], in0=hst[:, c0:c0 + CHUNK], scalar1=a_f[:, m, 1:2], scalar2=b2_f[:, m:m + 1], op0=ALU.mult, op1=ALU.add)
+                nc.vector.tensor_scalar(out=p2t[:, c0:c0 + CHUNK], in0=hst[:, c0:c0 + CHUNK], scalar1=a_f[:, m, 2:3], scalar2=None, op0=ALU.mult)
+                return
             nc.vector.scalar_tensor_tensor(out=vrow[(b, m)][:, 1 + c0 + lo:1 + c0 + hi], in0=h_t[(c, m)][:, lo:hi], scalar=a_f[:, m, 1:2],
                                            in1=g0row[(b, m)][:, c0 + lo:c0 + hi], op0=ALU.mult, op1=ALU.add)
 
         def zz(c, m, lo=0, hi=CHUNK):
             b, c0 = c // 2, (c % 2) * CHUNK
-            if m in BETA[b]:
+            if m in BETA[b] or m in XROW[b]:
                 return
             nc.vector.scalar_tensor_tensor(out=yrow[(b, m)][:, PADY - 1 + c0 + lo:PADY - 1 + c0 + hi], in0=h_t[(c, m)][:, lo:hi], scalar=a_f[:, m, 2:3],
                                            in1=vrow[(b, m)][:, c0 + lo:c0 + hi], op0=ALU.mult, op1=ALU.add)
@@ -168,7 +190,12 @@ def tile_cvim_pa_kernel(tc, x_bytes, x_scale, w1, b1, w2, b2, out):
             if (b, i) not in yT_t:
                 yT_t[(b, i)] = pst.tile([P, MT, P], F32, tag="t", name="yT")
             yT = yT_t[(b, i)]
-            if m in BETA[b]:
+            if m in XROW[b]:
+                hst, p0t, p1t, p2t = xrow[(b, m)]
+                nc.tensor.matmul(out=yT[:, m, :], lhsT=p0t[:, t0:t0 + P], rhs=ident[:], is_transpose=True, start=True, stop=False)
+                nc.tensor.matmul(out=yT[:, m, :], lhsT=p1t[:, t0:t0 + P], rhs=ident[:], is_transpose=True, start=False, stop=False)
+                nc.tensor.matmul(out=yT[:, m, :], lhsT=p2t[:, t0 + 1:t0 + 1 + P], rhs=ident[:], is_transpose=True, start=False, stop=True)
+            elif m in BETA[b]:
                 nc.tensor.matmul(out=yT[:, m, :], lhsT=vrow[(b, m)][:, 1 + t0:1 + t0 + P], rhs=ident[:], is_transpose=True, start=True, stop=False)
                 nc.tensor.matmul(out=yT[:, m, :], lhsT=yrow[(b, m)][:, PADY + t0:PADY + t0 + P], rhs=ident[:], is_transpose=True, start=False, stop=True)
             else:
@@ -197,10 +224,10 @@ def tile_cvim_pa_kernel(tc, x_bytes, x_scale, w1, b1, w2, b2, out):
                 ey(b, i, engs[j % len(engs)])
 
         widen(0)
-        turn(w_sb, wg, 0, False)
-        turn(w_sb, wg, 1, False)
         turn(xw_t[0], xg_t[0], 0)
         turn(xw_t[0], xg_t[0], 1)
+        turn(w_sb, wg, 0, False)
+        turn(w_sb, wg, 1, False)
         nc.vector.quantize_mx(out=wc[:].bitcast(FP8X4), scales=ws[:], in_=wg[:].rearrange("p n j -> p (n j)"))
         quant(0)
         widen(1)

@@ -22,9 +22,12 @@ PADY = 16
 FLOPS = 2 * NB * T * C * D + 6 * NB * T * D
 
 
-CAST = ("bb", "ss", "ss", "ss")
+CAST = ("sp", "ss", "ss", "pp")
+EYPAT = "sssssssssssvsvsv"
+DRAIN = ((0, 0, 0, 0), (3, 0, 0, 0), (5, 0, 0, 0), (3, 0, 0, 0))
 XROW = ((), ())
-BETA = ((2, 3), (3,))
+CROW = ((), ())
+BETA = ((0, 1, 2, 3), ())
 
 
 def tile_cvim_pa_kernel(tc, x_bytes, x_scale, w1, b1, w2, b2, out):
@@ -39,8 +42,14 @@ def tile_cvim_pa_kernel(tc, x_bytes, x_scale, w1, b1, w2, b2, out):
         psh = ctx.enter_context(tc.psum_pool(name="psh", bufs=1))
         pst = ctx.enter_context(tc.psum_pool(name="pst", bufs=4))
 
+        a_bf = const.tile([P, MT, 3], BF16, name="a_bf")
+        nc.sync.dma_start(out=a_bf[:], in_=w2.rearrange("(p m) j -> p m j", m=MT))
+        b1_bf = const.tile([P, MT], BF16, name="b1_bf")
+        nc.sync.dma_start(out=b1_bf[:], in_=b1.rearrange("(p m) -> p m", m=MT))
+        b2_bf = const.tile([P, MT], BF16, name="b2_bf")
+        nc.sync.dma_start(out=b2_bf[:], in_=b2.rearrange("(p m) -> p m", m=MT))
         s_kp = const.tile([P, 4], F32, name="s_kp")
-        nc.scalar.dma_start(out=s_kp[:], in_=x_scale.rearrange("a b (p t) -> (a b p) t", t=4))
+        nc.sync.dma_start(out=s_kp[:], in_=x_scale.rearrange("a b (p t) -> (a b p) t", t=4))
         xb = []
         for c in range(NCH):
             xbt = const.tile([P, 4, C], U8, name="xbytes%d" % c)
@@ -51,15 +60,11 @@ def tile_cvim_pa_kernel(tc, x_bytes, x_scale, w1, b1, w2, b2, out):
         nc.sync.dma_start(out=w_sb[:], in_=w1.rearrange("(p m) k -> p m k", m=MT))
         for c in range(1, NCH):
             nc.sync.dma_start(out=xb[c][:], in_=xflat[c * CHUNK:(c + 1) * CHUNK, :].rearrange("(i p) k -> p i k", p=P))
-        a_bf = const.tile([P, MT, 3], BF16, name="a_bf")
-        nc.scalar.dma_start(out=a_bf[:], in_=w2.rearrange("(p m) j -> p m j", m=MT))
-        b1_bf = const.tile([P, MT], BF16, name="b1_bf")
-        nc.scalar.dma_start(out=b1_bf[:], in_=b1.rearrange("(p m) -> p m", m=MT))
-        b2_bf = const.tile([P, MT], BF16, name="b2_bf")
-        nc.scalar.dma_start(out=b2_bf[:], in_=b2.rearrange("(p m) -> p m", m=MT))
 
         ident = const.tile([P, P], F32, name="ident")
         masks.make_identity(nc, ident[:])
+        ones = const.tile([P, 1], F32, name="ones")
+        nc.vector.memset(ones[:], 1.0)
         warm = const.tile([P, 2], F32, name="warm")
         nc.vector.memset(warm[:, 0:1], 0.0)
         nc.scalar.activation(out=warm[:, 1:2], in_=warm[:, 0:1], func=ACT.Identity)
@@ -101,7 +106,7 @@ def tile_cvim_pa_kernel(tc, x_bytes, x_scale, w1, b1, w2, b2, out):
                 vrow[(b, m)] = vt
                 yrow[(b, m)] = yt
                 nc.gpsimd.tensor_copy(out=g0t[:, 0:1], in_=pad0[:, m:m + 1])
-                if m in BETA[b]:
+                if m in BETA[b] or m in CROW[b]:
                     nc.gpsimd.tensor_copy(out=yt[:, PADY - 1 + T:PADY + T], in_=na2b1[:, m:m + 1])
                 else:
                     nc.vector.memset(vt[:, 0:1], 0.0)
@@ -118,6 +123,11 @@ def tile_cvim_pa_kernel(tc, x_bytes, x_scale, w1, b1, w2, b2, out):
 
         def widen(c):
             for hf in range(2):
+                if CAST[c][hf] == "p":
+                    nc.vector.tensor_scalar(out=xw_t[c][:, 2 * hf:2 * hf + 2, :].rearrange("p i k -> p (i k)").rearrange("p (u n e) -> p n u e", u=2, e=2),
+                                            in0=xb[c][:, 2 * hf:2 * hf + 2, :].rearrange("p i k -> p (i k)").bitcast(FP8).rearrange("p (n u e) -> p n u e", u=2, e=2),
+                                            scalar1=ones[:, 0:1], scalar2=None, op0=ALU.mult)
+                    continue
                 if CAST[c][hf] == "b":
                     nc.scalar.copy(out=xw_t[c][:, 2 * hf, :], in_=xb[c][:, 2 * hf, :].bitcast(FP8))
                     nc.vector.tensor_copy(out=xw_t[c][:, 2 * hf + 1, :], in_=xb[c][:, 2 * hf + 1, :].bitcast(FP8))
@@ -126,15 +136,21 @@ def tile_cvim_pa_kernel(tc, x_bytes, x_scale, w1, b1, w2, b2, out):
                 src = xb[c][:, 2 * hf:2 * hf + 2, :].rearrange("p i k -> p (i k)").bitcast(FP8)
                 if CAST[c][hf] == "s":
                     nc.scalar.copy(out=dst, in_=src)
+                elif CAST[c][hf] == "a":
+                    nc.any.tensor_copy(out=dst, in_=src)
                 else:
                     nc.vector.tensor_copy(out=dst, in_=src)
 
-        def turn(src, dst3, pair, scaled=True):
+        def turn(src, dst3, pair, scaled=True, perm=False):
             xt = pst.tile([P, 2, 2, P], F32, tag="t")
             for i2 in range(2):
                 words = src[:, 2 * pair + i2, :].bitcast(F32)
+                pwords = src[:, 2 * pair:2 * pair + 2, :].rearrange("p i k -> p (i k)").bitcast(F32)
                 for u in range(2):
-                    nc.tensor.transpose(xt[:, u, i2, :] if scaled else xt[:, i2, u, :], words[:, u:C // 2:2], ident[:])
+                    if perm:
+                        nc.tensor.transpose(xt[:, u, i2, :], pwords[:, (2 * u + i2) * P:(2 * u + i2 + 1) * P], ident[:])
+                    else:
+                        nc.tensor.transpose(xt[:, u, i2, :] if scaled else xt[:, i2, u, :], words[:, u:C // 2:2], ident[:])
             if scaled:
                 n0 = 2 * pair * P
                 nc.vector.tensor_tensor(out=dst3[:, n0:n0 + 2 * P, :].rearrange("p n (u e) -> p n u e", u=2),
@@ -160,24 +176,31 @@ def tile_cvim_pa_kernel(tc, x_bytes, x_scale, w1, b1, w2, b2, out):
                 return
             nc.scalar.activation(out=g0row[(b, m)][:, 1 + c0:1 + c0 + CHUNK], in_=h_t[(c, m)][:], func=ACT.Identity,
                                  scale=a_f[:, m, 0:1], bias=kall[:, m:m + 1])
-            if m in BETA[b]:
+            if m in BETA[b] or m in CROW[b]:
                 nc.scalar.activation(out=yrow[(b, m)][:, PADY - 1 + c0:PADY - 1 + c0 + CHUNK], in_=h_t[(c, m)][:], func=ACT.Identity,
                                      scale=a_f[:, m, 2:3])
+            if m in CROW[b]:
+                nc.scalar.activation(out=vrow[(b, m)][:, 1 + c0:1 + c0 + CHUNK], in_=h_t[(c, m)][:], func=ACT.Identity,
+                                     scale=a_f[:, m, 1:2])
 
         def vv(c, m, lo=0, hi=CHUNK):
             b, c0 = c // 2, (c % 2) * CHUNK
             if m in XROW[b]:
+                if c0 == 0:
+                    return
                 hst, p0t, p1t, p2t = xrow[(b, m)]
-                nc.vector.tensor_scalar(out=p0t[:, 1 + c0:1 + c0 + CHUNK], in0=hst[:, c0:c0 + CHUNK], scalar1=a_f[:, m, 0:1], scalar2=None, op0=ALU.mult)
-                nc.vector.tensor_scalar(out=p1t[:, c0:c0 + CHUNK], in0=hst[:, c0:c0 + CHUNK], scalar1=a_f[:, m, 1:2], scalar2=b2_f[:, m:m + 1], op0=ALU.mult, op1=ALU.add)
-                nc.vector.tensor_scalar(out=p2t[:, c0:c0 + CHUNK], in0=hst[:, c0:c0 + CHUNK], scalar1=a_f[:, m, 2:3], scalar2=None, op0=ALU.mult)
+                nc.vector.tensor_scalar(out=p0t[:, 1:1 + T], in0=hst[:], scalar1=a_f[:, m, 0:1], scalar2=None, op0=ALU.mult)
+                nc.vector.tensor_scalar(out=p1t[:], in0=hst[:], scalar1=a_f[:, m, 1:2], scalar2=b2_f[:, m:m + 1], op0=ALU.mult, op1=ALU.add)
+                nc.vector.tensor_scalar(out=p2t[:, 0:T], in0=hst[:], scalar1=a_f[:, m, 2:3], scalar2=None, op0=ALU.mult)
+                return
+            if m in CROW[b]:
                 return
             nc.vector.scalar_tensor_tensor(out=vrow[(b, m)][:, 1 + c0 + lo:1 + c0 + hi], in0=h_t[(c, m)][:, lo:hi], scalar=a_f[:, m, 1:2],
                                            in1=g0row[(b, m)][:, c0 + lo:c0 + hi], op0=ALU.mult, op1=ALU.add)
 
         def zz(c, m, lo=0, hi=CHUNK):
             b, c0 = c // 2, (c % 2) * CHUNK
-            if m in BETA[b] or m in XROW[b]:
+            if m in BETA[b] or m in CROW[b] or m in XROW[b]:
                 return
             nc.vector.scalar_tensor_tensor(out=yrow[(b, m)][:, PADY - 1 + c0 + lo:PADY - 1 + c0 + hi], in0=h_t[(c, m)][:, lo:hi], scalar=a_f[:, m, 2:3],
                                            in1=vrow[(b, m)][:, c0 + lo:c0 + hi], op0=ALU.mult, op1=ALU.add)
@@ -195,8 +218,10 @@ def tile_cvim_pa_kernel(tc, x_bytes, x_scale, w1, b1, w2, b2, out):
                 nc.tensor.matmul(out=yT[:, m, :], lhsT=p0t[:, t0:t0 + P], rhs=ident[:], is_transpose=True, start=True, stop=False)
                 nc.tensor.matmul(out=yT[:, m, :], lhsT=p1t[:, t0:t0 + P], rhs=ident[:], is_transpose=True, start=False, stop=False)
                 nc.tensor.matmul(out=yT[:, m, :], lhsT=p2t[:, t0 + 1:t0 + 1 + P], rhs=ident[:], is_transpose=True, start=False, stop=True)
-            elif m in BETA[b]:
-                nc.tensor.matmul(out=yT[:, m, :], lhsT=vrow[(b, m)][:, 1 + t0:1 + t0 + P], rhs=ident[:], is_transpose=True, start=True, stop=False)
+            elif m in BETA[b] or m in CROW[b]:
+                if m in CROW[b]:
+                    nc.tensor.matmul(out=yT[:, m, :], lhsT=g0row[(b, m)][:, t0:t0 + P], rhs=ident[:], is_transpose=True, start=True, stop=False)
+                nc.tensor.matmul(out=yT[:, m, :], lhsT=vrow[(b, m)][:, 1 + t0:1 + t0 + P], rhs=ident[:], is_transpose=True, start=m not in CROW[b], stop=False)
                 nc.tensor.matmul(out=yT[:, m, :], lhsT=yrow[(b, m)][:, PADY + t0:PADY + t0 + P], rhs=ident[:], is_transpose=True, start=False, stop=True)
             else:
                 nc.tensor.transpose(yT[:, m, :], yrow[(b, m)][:, PADY + t0:PADY + t0 + P], ident[:])
@@ -211,21 +236,24 @@ def tile_cvim_pa_kernel(tc, x_bytes, x_scale, w1, b1, w2, b2, out):
             dst, src = ysb[:].rearrange("p (q m) -> p q m", m=MT), yT_t[(b, i)][:].rearrange("p m q -> p q m")
             if eng == "s":
                 nc.scalar.copy(out=dst, in_=src)
+            elif eng == "a":
+                nc.any.tensor_copy(out=dst, in_=src)
             else:
                 nc.vector.tensor_copy(out=dst, in_=src)
             nc.sync.dma_start(out=oflat[b * T + t0:b * T + t0 + P, :], in_=ysb[:])
 
-        def tiles_of(c):
-            return [(c // 2, i) for i in ([0, 1, 2] if c % 2 == 0 else [3, 4, 5, 6, 7])]
+        nxt = [0]
 
-        def back(c, engs):
-            for j, (b, i) in enumerate(tiles_of(c)):
+        def emit(n):
+            for j in range(n):
+                b, i = nxt[0] // 8, nxt[0] % 8
                 ty(b, i)
-                ey(b, i, engs[j % len(engs)])
+                ey(b, i, EYPAT[nxt[0]])
+                nxt[0] += 1
 
         widen(0)
-        turn(xw_t[0], xg_t[0], 0)
-        turn(xw_t[0], xg_t[0], 1)
+        turn(xw_t[0], xg_t[0], 0, True, CAST[0][0] == "p")
+        turn(xw_t[0], xg_t[0], 1, True, CAST[0][1] == "p")
         turn(w_sb, wg, 0, False)
         turn(w_sb, wg, 1, False)
         nc.vector.quantize_mx(out=wc[:].bitcast(FP8X4), scales=ws[:], in_=wg[:].rearrange("p n j -> p (n j)"))
@@ -237,37 +265,39 @@ def tile_cvim_pa_kernel(tc, x_bytes, x_scale, w1, b1, w2, b2, out):
         g0(0, 1)
         mm(0, 3)
         mm(0, 2)
-        turn(xw_t[1], xg_t[1], 0)
-        turn(xw_t[1], xg_t[1], 1)
+        turn(xw_t[1], xg_t[1], 0, True, CAST[1][0] == "p")
+        turn(xw_t[1], xg_t[1], 1, True, CAST[1][1] == "p")
         g0(0, 3)
         g0(0, 2)
         for c in range(NCH):
-            nxt = c + 1 < NCH
+            more = c + 1 < NCH
             vv(c, 0)
             vv(c, 1)
             zz(c, 0)
-            if c > 0:
-                back(c - 1, "s")
-            if nxt:
+            emit(DRAIN[c][0])
+            if more:
                 quant(c + 1)
                 mm(c + 1, 0)
                 g0(c + 1, 0)
             if c + 2 < NCH:
                 widen(c + 2)
-                turn(xw_t[c + 2], xg_t[c + 2], 0)
-                turn(xw_t[c + 2], xg_t[c + 2], 1)
+                turn(xw_t[c + 2], xg_t[c + 2], 0, True, CAST[c + 2][0] == "p")
+                turn(xw_t[c + 2], xg_t[c + 2], 1, True, CAST[c + 2][1] == "p")
             vv(c, 2)
             zz(c, 1)
-            if nxt:
+            if more:
                 mm(c + 1, 1)
                 g0(c + 1, 1)
+            emit(DRAIN[c][1])
             vv(c, 3)
             zz(c, 3)
-            if nxt:
+            if more:
                 mm(c + 1, 3)
                 g0(c + 1, 3)
+            emit(DRAIN[c][2])
             zz(c, 2)
-            if nxt:
+            if more:
                 mm(c + 1, 2)
                 g0(c + 1, 2)
-        back(NCH - 1, "sv")
+            emit(DRAIN[c][3])
+        emit(16 - nxt[0])

@@ -23,7 +23,8 @@ FLOPS = 2 * NB * T * C * D + 6 * NB * T * D
 
 
 CAST = ("sp", "ss", "ss", "pp")
-EYPAT = "sssssssssssvsvsv"
+NSPLIT = 2
+EYPAT = "ssssssssssssssvs"
 DRAIN = ((0, 0, 0, 0), (3, 0, 0, 0), (5, 0, 0, 0), (3, 0, 0, 0))
 XROW = ((), ())
 CROW = ((), ())
@@ -271,6 +272,16 @@ def tile_cvim_pa_kernel(tc, x_bytes, x_scale, w1, b1, w2, b2, out):
         g0(0, 2)
         for c in range(NCH):
             more = c + 1 < NCH
+            if not more:
+                emit(DRAIN[c][0])
+                for piece in range(NSPLIT):
+                    lo, hi = piece * CHUNK // NSPLIT, (piece + 1) * CHUNK // NSPLIT
+                    for m in range(MT):
+                        vv(c, m, lo, hi)
+                    for m in range(MT):
+                        zz(c, m, lo, hi)
+                    emit(8 + (CHUNK + hi - 1) // P - nxt[0] if hi < CHUNK else 0)
+                continue
             vv(c, 0)
             vv(c, 1)
             zz(c, 0)

@@ -23,7 +23,7 @@ FLOPS = 2 * NB * T * C * D + 6 * NB * T * D
 
 
 CAST = ("sp", "ss", "ss", "pp")
-NSPLIT = 2
+PIECES = ((0, 256), (256, 384), (384, 512))
 EYPAT = "ssssssssssssssvs"
 DRAIN = ((0, 0, 0, 0), (3, 0, 0, 0), (5, 0, 0, 0), (3, 0, 0, 0))
 XROW = ((), ())
@@ -107,10 +107,12 @@ def tile_cvim_pa_kernel(tc, x_bytes, x_scale, w1, b1, w2, b2, out):
                 vrow[(b, m)] = vt
                 yrow[(b, m)] = yt
                 nc.gpsimd.tensor_copy(out=g0t[:, 0:1], in_=pad0[:, m:m + 1])
-                if m in BETA[b] or m in CROW[b]:
-                    nc.gpsimd.tensor_copy(out=yt[:, PADY - 1 + T:PADY + T], in_=na2b1[:, m:m + 1])
-                else:
+                if m not in BETA[b] and m not in CROW[b]:
                     nc.vector.memset(vt[:, 0:1], 0.0)
+        for b in range(NB):
+            for m in range(MT):
+                if m in BETA[b] or m in CROW[b]:
+                    nc.gpsimd.tensor_copy(out=yrow[(b, m)][:, PADY - 1 + T:PADY + T], in_=na2b1[:, m:m + 1])
 
         wg = const.tile([P, D, 4], BF16, name="wg", align_bytes=64)
         wc = const.tile([P, D], U32, name="wc", align_bytes=64)
@@ -264,18 +266,17 @@ def tile_cvim_pa_kernel(tc, x_bytes, x_scale, w1, b1, w2, b2, out):
         g0(0, 0)
         mm(0, 1)
         g0(0, 1)
-        mm(0, 3)
         mm(0, 2)
+        mm(0, 3)
         turn(xw_t[1], xg_t[1], 0, True, CAST[1][0] == "p")
         turn(xw_t[1], xg_t[1], 1, True, CAST[1][1] == "p")
-        g0(0, 3)
         g0(0, 2)
+        g0(0, 3)
         for c in range(NCH):
             more = c + 1 < NCH
             if not more:
                 emit(DRAIN[c][0])
-                for piece in range(NSPLIT):
-                    lo, hi = piece * CHUNK // NSPLIT, (piece + 1) * CHUNK // NSPLIT
+                for lo, hi in PIECES:
                     for m in range(MT):
                         vv(c, m, lo, hi)
                     for m in range(MT):
@@ -301,14 +302,14 @@ def tile_cvim_pa_kernel(tc, x_bytes, x_scale, w1, b1, w2, b2, out):
                 g0(c + 1, 1)
             emit(DRAIN[c][1])
             vv(c, 3)
-            zz(c, 3)
-            if more:
-                mm(c + 1, 3)
-                g0(c + 1, 3)
-            emit(DRAIN[c][2])
             zz(c, 2)
             if more:
                 mm(c + 1, 2)
                 g0(c + 1, 2)
+            emit(DRAIN[c][2])
+            zz(c, 3)
+            if more:
+                mm(c + 1, 3)
+                g0(c + 1, 3)
             emit(DRAIN[c][3])
         emit(16 - nxt[0])

@@ -22,7 +22,7 @@ PADY = 16
 FLOPS = 2 * NB * T * C * D + 6 * NB * T * D
 
 
-CAST = ("sp", "ss", "ss", "pp")
+CAST = ("sp", "ss", "gg", "gg")
 PIECES = ((0, 256), (256, 384), (384, 512))
 EYPAT = "ssssssssssssssvs"
 DRAIN = ((0, 0, 0, 0), (3, 0, 0, 0), (5, 0, 0, 0), (3, 0, 0, 0))
@@ -37,6 +37,7 @@ def tile_cvim_pa_kernel(tc, x_bytes, x_scale, w1, b1, w2, b2, out):
     oflat = out.rearrange("b t d -> (b t) d")
 
     with ExitStack() as ctx:
+        ctx.enter_context(tc.manual_schedule(engines={mybir.EngineType.Pool}))
         const = ctx.enter_context(tc.tile_pool(name="const", bufs=1))
         rows = ctx.enter_context(tc.tile_pool(name="rows", bufs=1))
         outp = ctx.enter_context(tc.tile_pool(name="outp", bufs=16))
@@ -88,6 +89,11 @@ def tile_cvim_pa_kernel(tc, x_bytes, x_scale, w1, b1, w2, b2, out):
         nc.gpsimd.tensor_tensor(out=na2b1[:], in0=a_f[:, :, 2], in1=b1_f[:], op=ALU.mult)
         nc.gpsimd.tensor_scalar(out=na2b1[:], in0=na2b1[:], scalar1=-1.0, scalar2=0.0, op0=ALU.mult, op1=ALU.add)
 
+        g0all = rows.tile([P, NB, MT, 1 + T], F32, name="g0all")
+        yall = rows.tile([P, NB, MT, PADY + T], F32, name="yall")
+        nc.gpsimd.tensor_copy(out=g0all[:, :, :, 0], in_=pad0[:].unsqueeze(1).to_broadcast([P, NB, MT]))
+        nc.gpsimd.tensor_copy(out=yall[:, 0, :, PADY - 1 + T], in_=na2b1[:])
+
         g0row, vrow, yrow, xrow = {}, {}, {}, {}
         for b in range(NB):
             for m in range(MT):
@@ -100,20 +106,12 @@ def tile_cvim_pa_kernel(tc, x_bytes, x_scale, w1, b1, w2, b2, out):
                     nc.vector.memset(p0t[:, 0:1], 0.0)
                     nc.vector.memset(p2t[:, T:T + 1], 0.0)
                     continue
-                g0t = rows.tile([P, 1 + T], F32, name="g0_%d_%d" % (b, m))
                 vt = rows.tile([P, 1 + T], F32, name="v_%d_%d" % (b, m))
-                yt = rows.tile([P, PADY + T], F32, name="y_%d_%d" % (b, m))
-                g0row[(b, m)] = g0t
+                g0row[(b, m)] = g0all[:, b, m, :]
                 vrow[(b, m)] = vt
-                yrow[(b, m)] = yt
-                nc.gpsimd.tensor_copy(out=g0t[:, 0:1], in_=pad0[:, m:m + 1])
+                yrow[(b, m)] = yall[:, b, m, :]
                 if m not in BETA[b] and m not in CROW[b]:
                     nc.vector.memset(vt[:, 0:1], 0.0)
-        for b in range(NB):
-            for m in range(MT):
-                if m in BETA[b] or m in CROW[b]:
-                    nc.gpsimd.tensor_copy(out=yrow[(b, m)][:, PADY - 1 + T:PADY + T], in_=na2b1[:, m:m + 1])
-
         wg = const.tile([P, D, 4], BF16, name="wg", align_bytes=64)
         wc = const.tile([P, D], U32, name="wc", align_bytes=64)
         ws = const.tile([P, D], U8, name="ws", align_bytes=64)
@@ -139,8 +137,8 @@ def tile_cvim_pa_kernel(tc, x_bytes, x_scale, w1, b1, w2, b2, out):
                 src = xb[c][:, 2 * hf:2 * hf + 2, :].rearrange("p i k -> p (i k)").bitcast(FP8)
                 if CAST[c][hf] == "s":
                     nc.scalar.copy(out=dst, in_=src)
-                elif CAST[c][hf] == "a":
-                    nc.any.tensor_copy(out=dst, in_=src)
+                elif CAST[c][hf] == "g":
+                    nc.gpsimd.tensor_copy(out=dst, in_=src)
                 else:
                     nc.vector.tensor_copy(out=dst, in_=src)
 

@@ -11,6 +11,7 @@ FP8 = mybir.dt.float8_e4m3fn
 FP8X4 = mybir.dt.float8_e4m3fn_x4
 ALU = mybir.AluOpType
 ACT = mybir.ActivationFunctionType
+ENG = mybir.EngineType
 
 NB, T, C, D = 2, 1024, 512, 512
 P = 128
@@ -21,14 +22,11 @@ PADY = 16
 
 FLOPS = 2 * NB * T * C * D + 6 * NB * T * D
 
-
-CAST = ("sp", "ss", "gg", "gg")
+CAST = ("ps", "sg", "sg", "gg")
+FORM = ("bbbG", "ssss")
 PIECES = ((0, 256), (256, 384), (384, 512))
 EYPAT = "ssssssssssssssvs"
-DRAIN = ((0, 0, 0, 0), (3, 0, 0, 0), (5, 0, 0, 0), (3, 0, 0, 0))
-XROW = ((), ())
-CROW = ((), ())
-BETA = ((0, 1, 2, 3), ())
+DRAIN = ((0, 0, 0, 0), (0, 0, 3, 0), (0, 3, 0, 2), (3, 0, 0, 0))
 
 
 def tile_cvim_pa_kernel(tc, x_bytes, x_scale, w1, b1, w2, b2, out):
@@ -37,7 +35,6 @@ def tile_cvim_pa_kernel(tc, x_bytes, x_scale, w1, b1, w2, b2, out):
     oflat = out.rearrange("b t d -> (b t) d")
 
     with ExitStack() as ctx:
-        ctx.enter_context(tc.manual_schedule(engines={mybir.EngineType.Pool}))
         const = ctx.enter_context(tc.tile_pool(name="const", bufs=1))
         rows = ctx.enter_context(tc.tile_pool(name="rows", bufs=1))
         outp = ctx.enter_context(tc.tile_pool(name="outp", bufs=16))
@@ -45,191 +42,148 @@ def tile_cvim_pa_kernel(tc, x_bytes, x_scale, w1, b1, w2, b2, out):
         pst = ctx.enter_context(tc.psum_pool(name="pst", bufs=4))
 
         a_bf = const.tile([P, MT, 3], BF16, name="a_bf")
-        nc.sync.dma_start(out=a_bf[:], in_=w2.rearrange("(p m) j -> p m j", m=MT))
         b1_bf = const.tile([P, MT], BF16, name="b1_bf")
-        nc.sync.dma_start(out=b1_bf[:], in_=b1.rearrange("(p m) -> p m", m=MT))
         b2_bf = const.tile([P, MT], BF16, name="b2_bf")
-        nc.sync.dma_start(out=b2_bf[:], in_=b2.rearrange("(p m) -> p m", m=MT))
         s_kp = const.tile([P, 4], F32, name="s_kp")
-        nc.sync.dma_start(out=s_kp[:], in_=x_scale.rearrange("a b (p t) -> (a b p) t", t=4))
-        xb = []
+        w_sb = const.tile([P, MT, C], BF16, name="w_sb")
+        wg = const.tile([P, D, 4], BF16, name="wg", align_bytes=64)
+        wc = const.tile([P, D], U32, name="wc", align_bytes=64)
+        ws = const.tile([P, D], U8, name="ws", align_bytes=64)
+        ident = const.tile([P, P], F32, name="ident")
+        ones = const.tile([P, 1], F32, name="ones")
+        warm = const.tile([P, 2], F32, name="warm")
+        xb, xw, xg, xc, xs, h_t, yT_t = [], [], [], [], [], {}, {}
         for c in range(NCH):
             xbt = const.tile([P, 4, C], U8, name="xbytes%d" % c)
+            xwt = const.tile([P, 4, C], BF16, name="xw%d" % c)
+            xgt = const.tile([P, CHUNK, 4], BF16, name="xg%d" % c, align_bytes=64)
+            xct = const.tile([P, CHUNK], U32, name="xc%d" % c, align_bytes=64)
+            xst = const.tile([P, CHUNK], U8, name="xs%d" % c, align_bytes=64)
             xb.append(xbt)
+            xw.append(xwt)
+            xg.append(xgt)
+            xc.append(xct)
+            xs.append(xst)
+        row0 = rows.tile([P, NB, MT, 1 + T], F32, name="row0")
+        row1 = rows.tile([P, NB, MT, 1 + T], F32, name="row1")
+        row2 = rows.tile([P, NB, MT, PADY + T], F32, name="row2")
+        hrow = {}
+        for b in range(NB):
+            for m in range(MT):
+                if FORM[b][m] in "gG":
+                    hrow[(b, m)] = rows.tile([P, T], F32, name="h_%d_%d" % (b, m))
+
         for hf in range(2):
             nc.sync.dma_start(out=xb[0][:, 2 * hf:2 * hf + 2, :], in_=xflat[hf * 2 * P:(hf + 1) * 2 * P, :].rearrange("(i p) k -> p i k", p=P))
-        w_sb = const.tile([P, MT, C], BF16, name="w_sb")
+        nc.sync.dma_start(out=s_kp[:], in_=x_scale.rearrange("a b (p t) -> (a b p) t", t=4))
+        nc.sync.dma_start(out=a_bf[:], in_=w2.rearrange("(p m) j -> p m j", m=MT))
+        nc.sync.dma_start(out=b1_bf[:], in_=b1.rearrange("(p m) -> p m", m=MT))
+        nc.sync.dma_start(out=b2_bf[:], in_=b2.rearrange("(p m) -> p m", m=MT))
         nc.sync.dma_start(out=w_sb[:], in_=w1.rearrange("(p m) k -> p m k", m=MT))
         for c in range(1, NCH):
             nc.sync.dma_start(out=xb[c][:], in_=xflat[c * CHUNK:(c + 1) * CHUNK, :].rearrange("(i p) k -> p i k", p=P))
 
-        ident = const.tile([P, P], F32, name="ident")
-        masks.make_identity(nc, ident[:])
-        ones = const.tile([P, 1], F32, name="ones")
-        nc.vector.memset(ones[:], 1.0)
-        warm = const.tile([P, 2], F32, name="warm")
-        nc.vector.memset(warm[:, 0:1], 0.0)
-        nc.scalar.activation(out=warm[:, 1:2], in_=warm[:, 0:1], func=ACT.Identity)
+        def widen(c, hf):
+            dst = xw[c][:, 2 * hf:2 * hf + 2, :].rearrange("p i k -> p (i k)")
+            src = xb[c][:, 2 * hf:2 * hf + 2, :].rearrange("p i k -> p (i k)").bitcast(FP8)
+            if CAST[c][hf] == "p":
+                nc.vector.tensor_scalar(out=dst.rearrange("p (u n e) -> p n u e", u=2, e=2), in0=src.rearrange("p (n u e) -> p n u e", u=2, e=2),
+                                        scalar1=ones[:, 0:1], scalar2=None, op0=ALU.mult)
+            elif CAST[c][hf] == "s":
+                nc.scalar.copy(out=dst, in_=src)
+            else:
+                nc.gpsimd.tensor_copy(out=dst, in_=src)
 
-        a_f = const.tile([P, MT, 3], F32, name="a_f")
-        nc.gpsimd.tensor_copy(out=a_f[:], in_=a_bf[:])
-        b1_f = const.tile([P, MT], F32, name="b1_f")
-        nc.gpsimd.tensor_copy(out=b1_f[:], in_=b1_bf[:])
-        b2_f = const.tile([P, MT], F32, name="b2_f")
-        nc.gpsimd.tensor_copy(out=b2_f[:], in_=b2_bf[:])
-        pad0 = const.tile([P, MT], F32, name="pad0")
-        kall = const.tile([P, MT], F32, name="kall")
-        na2b1 = const.tile([P, MT], F32, name="na2b1")
-        tmp = const.tile([P, MT], F32, name="tmp")
-        nc.gpsimd.tensor_tensor(out=pad0[:], in0=a_f[:, :, 1], in1=a_f[:, :, 2], op=ALU.add)
-        nc.gpsimd.tensor_tensor(out=pad0[:], in0=pad0[:], in1=b1_f[:], op=ALU.mult)
-        nc.gpsimd.tensor_tensor(out=pad0[:], in0=pad0[:], in1=b2_f[:], op=ALU.add)
-        nc.gpsimd.tensor_tensor(out=tmp[:], in0=a_f[:, :, 0], in1=b1_f[:], op=ALU.mult)
-        nc.gpsimd.tensor_tensor(out=kall[:], in0=pad0[:], in1=tmp[:], op=ALU.add)
-        nc.gpsimd.tensor_tensor(out=na2b1[:], in0=a_f[:, :, 2], in1=b1_f[:], op=ALU.mult)
-        nc.gpsimd.tensor_scalar(out=na2b1[:], in0=na2b1[:], scalar1=-1.0, scalar2=0.0, op0=ALU.mult, op1=ALU.add)
+        def words(src, pair):
+            return src[:, 2 * pair:2 * pair + 2, :].rearrange("p i k -> p (i k)").bitcast(F32)
 
-        g0all = rows.tile([P, NB, MT, 1 + T], F32, name="g0all")
-        yall = rows.tile([P, NB, MT, PADY + T], F32, name="yall")
-        nc.gpsimd.tensor_copy(out=g0all[:, :, :, 0], in_=pad0[:].unsqueeze(1).to_broadcast([P, NB, MT]))
-        nc.gpsimd.tensor_copy(out=yall[:, 0, :, PADY - 1 + T], in_=na2b1[:])
-
-        g0row, vrow, yrow, xrow = {}, {}, {}, {}
-        for b in range(NB):
-            for m in range(MT):
-                if m in XROW[b]:
-                    hst = rows.tile([P, T], F32, name="hs_%d_%d" % (b, m))
-                    p0t = rows.tile([P, 1 + T], F32, name="p0_%d_%d" % (b, m))
-                    p1t = rows.tile([P, T], F32, name="p1_%d_%d" % (b, m))
-                    p2t = rows.tile([P, T + 1], F32, name="p2_%d_%d" % (b, m))
-                    xrow[(b, m)] = (hst, p0t, p1t, p2t)
-                    nc.vector.memset(p0t[:, 0:1], 0.0)
-                    nc.vector.memset(p2t[:, T:T + 1], 0.0)
-                    continue
-                vt = rows.tile([P, 1 + T], F32, name="v_%d_%d" % (b, m))
-                g0row[(b, m)] = g0all[:, b, m, :]
-                vrow[(b, m)] = vt
-                yrow[(b, m)] = yall[:, b, m, :]
-                if m not in BETA[b] and m not in CROW[b]:
-                    nc.vector.memset(vt[:, 0:1], 0.0)
-        wg = const.tile([P, D, 4], BF16, name="wg", align_bytes=64)
-        wc = const.tile([P, D], U32, name="wc", align_bytes=64)
-        ws = const.tile([P, D], U8, name="ws", align_bytes=64)
-        xw_t, xg_t, xc_t, xs_t, h_t, yT_t, ysb_t = {}, {}, {}, {}, {}, {}, {}
-        for c in range(NCH):
-            xw_t[c] = const.tile([P, 4, C], BF16, name="xw%d" % c)
-            xg_t[c] = const.tile([P, CHUNK, 4], BF16, name="xg%d" % c, align_bytes=64)
-            xc_t[c] = const.tile([P, CHUNK], U32, name="xc%d" % c, align_bytes=64)
-            xs_t[c] = const.tile([P, CHUNK], U8, name="xs%d" % c, align_bytes=64)
-
-        def widen(c):
-            for hf in range(2):
-                if CAST[c][hf] == "p":
-                    nc.vector.tensor_scalar(out=xw_t[c][:, 2 * hf:2 * hf + 2, :].rearrange("p i k -> p (i k)").rearrange("p (u n e) -> p n u e", u=2, e=2),
-                                            in0=xb[c][:, 2 * hf:2 * hf + 2, :].rearrange("p i k -> p (i k)").bitcast(FP8).rearrange("p (n u e) -> p n u e", u=2, e=2),
-                                            scalar1=ones[:, 0:1], scalar2=None, op0=ALU.mult)
-                    continue
-                if CAST[c][hf] == "b":
-                    nc.scalar.copy(out=xw_t[c][:, 2 * hf, :], in_=xb[c][:, 2 * hf, :].bitcast(FP8))
-                    nc.vector.tensor_copy(out=xw_t[c][:, 2 * hf + 1, :], in_=xb[c][:, 2 * hf + 1, :].bitcast(FP8))
-                    continue
-                dst = xw_t[c][:, 2 * hf:2 * hf + 2, :].rearrange("p i k -> p (i k)")
-                src = xb[c][:, 2 * hf:2 * hf + 2, :].rearrange("p i k -> p (i k)").bitcast(FP8)
-                if CAST[c][hf] == "s":
-                    nc.scalar.copy(out=dst, in_=src)
-                elif CAST[c][hf] == "g":
-                    nc.gpsimd.tensor_copy(out=dst, in_=src)
-                else:
-                    nc.vector.tensor_copy(out=dst, in_=src)
-
-        def turn(src, dst3, pair, scaled=True, perm=False):
+        def turn_x(c, hf):
             xt = pst.tile([P, 2, 2, P], F32, tag="t")
             for i2 in range(2):
-                words = src[:, 2 * pair + i2, :].bitcast(F32)
-                pwords = src[:, 2 * pair:2 * pair + 2, :].rearrange("p i k -> p (i k)").bitcast(F32)
                 for u in range(2):
-                    if perm:
-                        nc.tensor.transpose(xt[:, u, i2, :], pwords[:, (2 * u + i2) * P:(2 * u + i2 + 1) * P], ident[:])
-                    else:
-                        nc.tensor.transpose(xt[:, u, i2, :] if scaled else xt[:, i2, u, :], words[:, u:C // 2:2], ident[:])
-            if scaled:
-                n0 = 2 * pair * P
-                nc.vector.tensor_tensor(out=dst3[:, n0:n0 + 2 * P, :].rearrange("p n (u e) -> p n u e", u=2),
-                                        in0=xt[:].rearrange("p u i r -> p (u i r)").bitcast(BF16).rearrange("p (u n e) -> p n u e", u=2, e=2),
-                                        in1=s_kp[:].rearrange("p (u e) -> p u e", u=2).unsqueeze(1).to_broadcast([P, 2 * P, 2, 2]), op=ALU.mult)
-            else:
-                dst = dst3[:, 2 * pair * P:(2 * pair + 2) * P, :].rearrange("p n j -> p (n j)").bitcast(F32)
-                nc.scalar.copy(out=dst.rearrange("p (i r u) -> p i r u", i=2, u=2), in_=xt[:].rearrange("p i u r -> p i r u"))
+                    lo = (2 * u + i2) * P if CAST[c][hf] == "p" else 2 * i2 * P + u
+                    step = 1 if CAST[c][hf] == "p" else 2
+                    nc.tensor.transpose(xt[:, u, i2, :], words(xw[c], hf)[:, lo:lo + (P - 1) * step + 1:step], ident[:])
+            return xt
+
+        def scale_x(c, hf, xt):
+            n0 = 2 * hf * P
+            nc.vector.tensor_tensor(out=xg[c][:, n0:n0 + 2 * P, :].rearrange("p n (u e) -> p n u e", u=2),
+                                    in0=xt[:].rearrange("p u i r -> p (u i r)").bitcast(BF16).rearrange("p (u n e) -> p n u e", u=2, e=2),
+                                    in1=s_kp[:].rearrange("p (u e) -> p u e", u=2).unsqueeze(1).to_broadcast([P, 2 * P, 2, 2]), op=ALU.mult)
+
+        def turn_w(pair):
+            wt = pst.tile([P, 2, 2, P], F32, tag="t")
+            for i2 in range(2):
+                for u in range(2):
+                    lo = 2 * i2 * P + u
+                    nc.tensor.transpose(wt[:, i2, u, :], words(w_sb, pair)[:, lo:lo + 2 * P - 1:2], ident[:])
+            dst = wg[:, 2 * pair * P:(2 * pair + 2) * P, :].rearrange("p n j -> p (n j)").bitcast(F32)
+            nc.scalar.copy(out=dst.rearrange("p (i r u) -> p i r u", i=2, u=2), in_=wt[:].rearrange("p i u r -> p i r u"))
+
+        def quant_w():
+            nc.vector.quantize_mx(out=wc[:].bitcast(FP8X4), scales=ws[:], in_=wg[:].rearrange("p n j -> p (n j)"))
 
         def quant(c):
-            nc.vector.quantize_mx(out=xc_t[c][:].bitcast(FP8X4), scales=xs_t[c][:], in_=xg_t[c][:].rearrange("p n j -> p (n j)"))
+            nc.vector.quantize_mx(out=xc[c][:].bitcast(FP8X4), scales=xs[c][:], in_=xg[c][:].rearrange("p n j -> p (n j)"))
 
         def mm(c, m):
             h = psh.tile([P, CHUNK], F32, tag="h%d" % m)
             h_t[(c, m)] = h
             nc.tensor.matmul_mx(out=h[:], lhsT=wc[:, m * P:(m + 1) * P].bitcast(FP8X4), lhsT_scale=ws[:, m * P:(m + 1) * P],
-                                rhs=xc_t[c][:].bitcast(FP8X4), rhs_scale=xs_t[c][:], start=True, stop=True)
+                                rhs=xc[c][:].bitcast(FP8X4), rhs_scale=xs[c][:], start=True, stop=True)
 
-        def g0(c, m):
+        def s_taps(c, m):
             b, c0 = c // 2, (c % 2) * CHUNK
-            if m in XROW[b]:
-                nc.scalar.activation(out=xrow[(b, m)][0][:, c0:c0 + CHUNK], in_=h_t[(c, m)][:], func=ACT.Identity, bias=b1_f[:, m:m + 1])
+            H = h_t[(c, m)][:]
+            if FORM[b][m] in "gG":
+                hr = hrow[(b, m)]
+                nc.scalar.activation(out=hr[:, c0:c0 + CHUNK], in_=H, func=ACT.Identity, bias=b1_f[:, m:m + 1])
+                if FORM[b][m] == "G":
+                    nc.scalar.activation(out=row1[:, b, m, 1 + c0:1 + c0 + CHUNK], in_=H, func=ACT.Identity, scale=a_f[:, m, 1:2], bias=k1[:, m:m + 1])
+                if FORM[b][m] in "gG":
+                    nc.gpsimd.tensor_tensor(out=row0[:, b, m, 1 + c0:1 + c0 + CHUNK], in0=hr[:, c0:c0 + CHUNK],
+                                            in1=a_f[:, m, 0:1].to_broadcast([P, CHUNK]), op=ALU.mult)
+                    nc.gpsimd.tensor_tensor(out=row2[:, b, m, PADY - 1 + c0:PADY - 1 + c0 + CHUNK], in0=hr[:, c0:c0 + CHUNK],
+                                            in1=a_f[:, m, 2:3].to_broadcast([P, CHUNK]), op=ALU.mult)
                 return
-            nc.scalar.activation(out=g0row[(b, m)][:, 1 + c0:1 + c0 + CHUNK], in_=h_t[(c, m)][:], func=ACT.Identity,
-                                 scale=a_f[:, m, 0:1], bias=kall[:, m:m + 1])
-            if m in BETA[b] or m in CROW[b]:
-                nc.scalar.activation(out=yrow[(b, m)][:, PADY - 1 + c0:PADY - 1 + c0 + CHUNK], in_=h_t[(c, m)][:], func=ACT.Identity,
-                                     scale=a_f[:, m, 2:3])
-            if m in CROW[b]:
-                nc.scalar.activation(out=vrow[(b, m)][:, 1 + c0:1 + c0 + CHUNK], in_=h_t[(c, m)][:], func=ACT.Identity,
-                                     scale=a_f[:, m, 1:2])
+            nc.scalar.activation(out=row0[:, b, m, 1 + c0:1 + c0 + CHUNK], in_=H, func=ACT.Identity, scale=a_f[:, m, 0:1], bias=kall[:, m:m + 1])
+            if FORM[b][m] == "b":
+                nc.scalar.activation(out=row2[:, b, m, PADY - 1 + c0:PADY - 1 + c0 + CHUNK], in_=H, func=ACT.Identity, scale=a_f[:, m, 2:3])
 
         def vv(c, m, lo=0, hi=CHUNK):
             b, c0 = c // 2, (c % 2) * CHUNK
-            if m in XROW[b]:
-                if c0 == 0:
-                    return
-                hst, p0t, p1t, p2t = xrow[(b, m)]
-                nc.vector.tensor_scalar(out=p0t[:, 1:1 + T], in0=hst[:], scalar1=a_f[:, m, 0:1], scalar2=None, op0=ALU.mult)
-                nc.vector.tensor_scalar(out=p1t[:], in0=hst[:], scalar1=a_f[:, m, 1:2], scalar2=b2_f[:, m:m + 1], op0=ALU.mult, op1=ALU.add)
-                nc.vector.tensor_scalar(out=p2t[:, 0:T], in0=hst[:], scalar1=a_f[:, m, 2:3], scalar2=None, op0=ALU.mult)
+            H = h_t[(c, m)][:, lo:hi]
+            if FORM[b][m] == "G":
                 return
-            if m in CROW[b]:
-                return
-            nc.vector.scalar_tensor_tensor(out=vrow[(b, m)][:, 1 + c0 + lo:1 + c0 + hi], in0=h_t[(c, m)][:, lo:hi], scalar=a_f[:, m, 1:2],
-                                           in1=g0row[(b, m)][:, c0 + lo:c0 + hi], op0=ALU.mult, op1=ALU.add)
+            if FORM[b][m] == "g":
+                nc.vector.tensor_scalar(out=row1[:, b, m, 1 + c0 + lo:1 + c0 + hi], in0=H, scalar1=a_f[:, m, 1:2], scalar2=k1[:, m:m + 1], op0=ALU.mult, op1=ALU.add)
+            else:
+                nc.vector.scalar_tensor_tensor(out=row1[:, b, m, 1 + c0 + lo:1 + c0 + hi], in0=H, scalar=a_f[:, m, 1:2],
+                                               in1=row0[:, b, m, c0 + lo:c0 + hi], op0=ALU.mult, op1=ALU.add)
 
         def zz(c, m, lo=0, hi=CHUNK):
             b, c0 = c // 2, (c % 2) * CHUNK
-            if m in BETA[b] or m in CROW[b] or m in XROW[b]:
+            if FORM[b][m] != "s":
                 return
-            nc.vector.scalar_tensor_tensor(out=yrow[(b, m)][:, PADY - 1 + c0 + lo:PADY - 1 + c0 + hi], in0=h_t[(c, m)][:, lo:hi], scalar=a_f[:, m, 2:3],
-                                           in1=vrow[(b, m)][:, c0 + lo:c0 + hi], op0=ALU.mult, op1=ALU.add)
+            nc.vector.scalar_tensor_tensor(out=row2[:, b, m, PADY - 1 + c0 + lo:PADY - 1 + c0 + hi], in0=h_t[(c, m)][:, lo:hi], scalar=a_f[:, m, 2:3],
+                                           in1=row1[:, b, m, c0 + lo:c0 + hi], op0=ALU.mult, op1=ALU.add)
             if c0 + hi == T:
-                nc.vector.tensor_scalar(out=yrow[(b, m)][:, PADY + T - 1:PADY + T], in0=vrow[(b, m)][:, T:T + 1],
+                nc.vector.tensor_scalar(out=row2[:, b, m, PADY + T - 1:PADY + T], in0=row1[:, b, m, T:T + 1],
                                         scalar1=na2b1[:, m:m + 1], scalar2=None, op0=ALU.add)
 
-        def ty_m(b, i, m):
-            t0 = i * P
-            if (b, i) not in yT_t:
-                yT_t[(b, i)] = pst.tile([P, MT, P], F32, tag="t", name="yT")
-            yT = yT_t[(b, i)]
-            if m in XROW[b]:
-                hst, p0t, p1t, p2t = xrow[(b, m)]
-                nc.tensor.matmul(out=yT[:, m, :], lhsT=p0t[:, t0:t0 + P], rhs=ident[:], is_transpose=True, start=True, stop=False)
-                nc.tensor.matmul(out=yT[:, m, :], lhsT=p1t[:, t0:t0 + P], rhs=ident[:], is_transpose=True, start=False, stop=False)
-                nc.tensor.matmul(out=yT[:, m, :], lhsT=p2t[:, t0 + 1:t0 + 1 + P], rhs=ident[:], is_transpose=True, start=False, stop=True)
-            elif m in BETA[b] or m in CROW[b]:
-                if m in CROW[b]:
-                    nc.tensor.matmul(out=yT[:, m, :], lhsT=g0row[(b, m)][:, t0:t0 + P], rhs=ident[:], is_transpose=True, start=True, stop=False)
-                nc.tensor.matmul(out=yT[:, m, :], lhsT=vrow[(b, m)][:, 1 + t0:1 + t0 + P], rhs=ident[:], is_transpose=True, start=m not in CROW[b], stop=False)
-                nc.tensor.matmul(out=yT[:, m, :], lhsT=yrow[(b, m)][:, PADY + t0:PADY + t0 + P], rhs=ident[:], is_transpose=True, start=False, stop=True)
-            else:
-                nc.tensor.transpose(yT[:, m, :], yrow[(b, m)][:, PADY + t0:PADY + t0 + P], ident[:])
-
         def ty(b, i):
+            t0 = i * P
+            yT = pst.tile([P, MT, P], F32, tag="t", name="yT")
+            yT_t[(b, i)] = yT
             for m in range(MT):
-                ty_m(b, i, m)
+                parts = [row2[:, b, m, PADY + t0:PADY + t0 + P]]
+                if FORM[b][m] != "s":
+                    parts = [row1[:, b, m, 1 + t0:1 + t0 + P]] + parts
+                if FORM[b][m] in "gG":
+                    parts = [row0[:, b, m, t0:t0 + P]] + parts
+                for n, part in enumerate(parts):
+                    nc.tensor.matmul(out=yT[:, m, :], lhsT=part, rhs=ident[:], is_transpose=True, start=n == 0, stop=n == len(parts) - 1)
 
         def ey(b, i, eng):
             t0 = i * P
@@ -237,8 +191,6 @@ def tile_cvim_pa_kernel(tc, x_bytes, x_scale, w1, b1, w2, b2, out):
             dst, src = ysb[:].rearrange("p (q m) -> p q m", m=MT), yT_t[(b, i)][:].rearrange("p m q -> p q m")
             if eng == "s":
                 nc.scalar.copy(out=dst, in_=src)
-            elif eng == "a":
-                nc.any.tensor_copy(out=dst, in_=src)
             else:
                 nc.vector.tensor_copy(out=dst, in_=src)
             nc.sync.dma_start(out=oflat[b * T + t0:b * T + t0 + P, :], in_=ysb[:])
@@ -252,24 +204,68 @@ def tile_cvim_pa_kernel(tc, x_bytes, x_scale, w1, b1, w2, b2, out):
                 ey(b, i, EYPAT[nxt[0]])
                 nxt[0] += 1
 
-        widen(0)
-        turn(xw_t[0], xg_t[0], 0, True, CAST[0][0] == "p")
-        turn(xw_t[0], xg_t[0], 1, True, CAST[0][1] == "p")
-        turn(w_sb, wg, 0, False)
-        turn(w_sb, wg, 1, False)
-        nc.vector.quantize_mx(out=wc[:].bitcast(FP8X4), scales=ws[:], in_=wg[:].rearrange("p n j -> p (n j)"))
-        quant(0)
-        widen(1)
-        mm(0, 0)
-        g0(0, 0)
-        mm(0, 1)
-        g0(0, 1)
-        mm(0, 2)
-        mm(0, 3)
-        turn(xw_t[1], xg_t[1], 0, True, CAST[1][0] == "p")
-        turn(xw_t[1], xg_t[1], 1, True, CAST[1][1] == "p")
-        g0(0, 2)
-        g0(0, 3)
+        with tc.manual_schedule(engines={ENG.Pool, ENG.DVE, ENG.PE, ENG.Activation}):
+            masks.make_identity(nc, ident[:])
+            nc.vector.memset(ones[:], 1.0)
+            nc.vector.memset(warm[:, 0:1], 0.0)
+            nc.scalar.activation(out=warm[:, 1:2], in_=warm[:, 0:1], func=ACT.Identity)
+            for b in range(NB):
+                for m in range(MT):
+                    if FORM[b][m] == "s":
+                        nc.vector.memset(row1[:, b, m, 0:1], 0.0)
+                    if FORM[b][m] in "gG":
+                        nc.vector.memset(row0[:, b, m, 0:1], 0.0)
+                        nc.vector.memset(row2[:, b, m, PADY + T - 1:PADY + T], 0.0)
+
+            a_f = const.tile([P, MT, 3], F32, name="a_f")
+            ab = const.tile([P, MT, 3], F32, name="ab")
+            b1_f = const.tile([P, MT], F32, name="b1_f")
+            k1 = const.tile([P, MT], F32, name="k1")
+            pad0 = const.tile([P, MT], F32, name="pad0")
+            kall = const.tile([P, MT], F32, name="kall")
+            na2b1 = const.tile([P, MT], F32, name="na2b1")
+            nc.gpsimd.tensor_copy(out=a_f[:], in_=a_bf[:])
+            nc.gpsimd.tensor_copy(out=b1_f[:], in_=b1_bf[:])
+            nc.gpsimd.tensor_tensor(out=ab[:], in0=a_f[:], in1=b1_f[:].unsqueeze(2).to_broadcast([P, MT, 3]), op=ALU.mult)
+            nc.gpsimd.tensor_tensor(out=k1[:], in0=ab[:, :, 1], in1=b2_bf[:], op=ALU.add)
+            nc.gpsimd.tensor_tensor(out=pad0[:], in0=ab[:, :, 2], in1=k1[:], op=ALU.add)
+            nc.gpsimd.tensor_tensor(out=kall[:], in0=ab[:, :, 0], in1=pad0[:], op=ALU.add)
+            for b in range(NB):
+                n = sum(f in "bs" for f in FORM[b])
+                nc.gpsimd.tensor_copy(out=row0[:, b, 0:n, 0], in_=pad0[:, 0:n])
+
+            widen(0, 0)
+            widen(0, 1)
+            widen(1, 0)
+            xt = turn_x(0, 0)
+            scale_x(0, 0, xt)
+            xt = turn_x(0, 1)
+            scale_x(0, 1, xt)
+            turn_w(0)
+            turn_w(1)
+            widen(1, 1)
+            widen(2, 0)
+            quant(0)
+            quant_w()
+            for hf in range(2):
+                xt = turn_x(1, hf)
+                scale_x(1, hf, xt)
+            mm(0, 0)
+            s_taps(0, 0)
+            mm(0, 1)
+            s_taps(0, 1)
+            mm(0, 2)
+            mm(0, 3)
+            widen(2, 1)
+            widen(3, 0)
+            widen(3, 1)
+            nc.gpsimd.tensor_scalar(out=na2b1[:], in0=ab[:, :, 2], scalar1=-1.0, scalar2=0.0, op0=ALU.mult, op1=ALU.add)
+            n = sum(f == "b" for f in FORM[0])
+            nc.gpsimd.tensor_copy(out=row2[:, 0, 0:n, PADY - 1 + T], in_=na2b1[:, 0:n])
+            xt2 = [turn_x(2, 0), turn_x(2, 1)]
+            quant(1)
+        s_taps(0, 2)
+        s_taps(0, 3)
         for c in range(NCH):
             more = c + 1 < NCH
             if not more:
@@ -285,29 +281,26 @@ def tile_cvim_pa_kernel(tc, x_bytes, x_scale, w1, b1, w2, b2, out):
             vv(c, 1)
             zz(c, 0)
             emit(DRAIN[c][0])
-            if more:
+            if c > 0:
                 quant(c + 1)
-                mm(c + 1, 0)
-                g0(c + 1, 0)
+            mm(c + 1, 0)
+            s_taps(c + 1, 0)
             if c + 2 < NCH:
-                widen(c + 2)
-                turn(xw_t[c + 2], xg_t[c + 2], 0, True, CAST[c + 2][0] == "p")
-                turn(xw_t[c + 2], xg_t[c + 2], 1, True, CAST[c + 2][1] == "p")
+                for hf in range(2):
+                    xt = xt2[hf] if c == 0 else turn_x(c + 2, hf)
+                    scale_x(c + 2, hf, xt)
             vv(c, 2)
             zz(c, 1)
-            if more:
-                mm(c + 1, 1)
-                g0(c + 1, 1)
+            mm(c + 1, 1)
+            s_taps(c + 1, 1)
             emit(DRAIN[c][1])
             vv(c, 3)
             zz(c, 2)
-            if more:
-                mm(c + 1, 2)
-                g0(c + 1, 2)
+            mm(c + 1, 2)
+            s_taps(c + 1, 2)
             emit(DRAIN[c][2])
             zz(c, 3)
-            if more:
-                mm(c + 1, 3)
-                g0(c + 1, 3)
+            mm(c + 1, 3)
+            s_taps(c + 1, 3)
             emit(DRAIN[c][3])
         emit(16 - nxt[0])

@@ -22,8 +22,8 @@ PADY = 16
 
 FLOPS = 2 * NB * T * C * D + 6 * NB * T * D
 
-CAST = ("ps", "sg", "sg", "gg")
-FORM = ("bbbG", "ssss")
+CAST = ("pp", "ss", "sg", "gg")
+FORM = ("bbbb", "ssss")
 PIECES = ((0, 256), (256, 384), (384, 512))
 EYPAT = "ssssssssssssssvs"
 DRAIN = ((0, 0, 0, 0), (0, 0, 3, 0), (0, 3, 0, 2), (3, 0, 0, 0))
@@ -231,8 +231,8 @@ def tile_cvim_pa_kernel(tc, x_bytes, x_scale, w1, b1, w2, b2, out):
             nc.gpsimd.tensor_tensor(out=pad0[:], in0=ab[:, :, 2], in1=k1[:], op=ALU.add)
             nc.gpsimd.tensor_tensor(out=kall[:], in0=ab[:, :, 0], in1=pad0[:], op=ALU.add)
             for b in range(NB):
-                n = sum(f in "bs" for f in FORM[b])
-                nc.gpsimd.tensor_copy(out=row0[:, b, 0:n, 0], in_=pad0[:, 0:n])
+                ms = [m for m in range(MT) if FORM[b][m] in "bs"]
+                nc.gpsimd.tensor_copy(out=row0[:, b, ms[0]:ms[-1] + 1, 0], in_=pad0[:, ms[0]:ms[-1] + 1])
 
             widen(0, 0)
             widen(0, 1)

@@ -23,7 +23,7 @@ PADY = 16
 FLOPS = 2 * NB * T * C * D + 6 * NB * T * D
 
 CAST = ("pp", "ss", "sg", "gg")
-FORM = ("bbbb", "ssss")
+FORM = ("bbbG", "ssss")
 PIECES = ((0, 256), (256, 384), (384, 512))
 EYPAT = "ssssssssssssssvs"
 DRAIN = ((0, 0, 0, 0), (0, 0, 3, 0), (0, 3, 0, 2), (3, 0, 0, 0))

@@ -24,6 +24,10 @@ FLOPS = 2 * NB * T * C * D + 6 * NB * T * D
 
 CAST = ("pp", "ss", "sg", "gg")
 FORM = ("bbbG", "ssss")
+XC = 1
+C0 = "ssss"
+GSC = ()
+XM = ((0, 1), (2, 3))
 PIECES = ((0, 256), (256, 384), (384, 512))
 EYPAT = "ssssssssssssssvs"
 DRAIN = ((0, 0, 0, 0), (0, 0, 3, 0), (0, 3, 0, 2), (3, 0, 0, 0))
@@ -70,7 +74,7 @@ def tile_cvim_pa_kernel(tc, x_bytes, x_scale, w1, b1, w2, b2, out):
         hrow = {}
         for b in range(NB):
             for m in range(MT):
-                if FORM[b][m] in "gG":
+                if FORM[b][m] in "gGx":
                     hrow[(b, m)] = rows.tile([P, T], F32, name="h_%d_%d" % (b, m))
 
         for hf in range(2):
@@ -103,14 +107,36 @@ def tile_cvim_pa_kernel(tc, x_bytes, x_scale, w1, b1, w2, b2, out):
                 for u in range(2):
                     lo = (2 * u + i2) * P if CAST[c][hf] == "p" else 2 * i2 * P + u
                     step = 1 if CAST[c][hf] == "p" else 2
-                    nc.tensor.transpose(xt[:, u, i2, :], words(xw[c], hf)[:, lo:lo + (P - 1) * step + 1:step], ident[:])
+                    nc.tensor.transpose(xt[:, i2, u, :] if (c, hf) in GSC else xt[:, u, i2, :], words(xw[c], hf)[:, lo:lo + (P - 1) * step + 1:step], ident[:])
             return xt
 
         def scale_x(c, hf, xt):
             n0 = 2 * hf * P
+            if (c, hf) in GSC:
+                raw = const.tile([P, 2 * P, 4], BF16, name="raw%d%d" % (c, hf))
+                nc.scalar.copy(out=raw[:].rearrange("p n j -> p (n j)").bitcast(F32).rearrange("p (i r u) -> p i r u", i=2, u=2), in_=xt[:].rearrange("p i u r -> p i r u"))
+                nc.gpsimd.tensor_tensor(out=xg[c][:, n0:n0 + 2 * P, :], in0=raw[:], in1=s_kp[:].unsqueeze(1).to_broadcast([P, 2 * P, 4]), op=ALU.mult)
+                return
             nc.vector.tensor_tensor(out=xg[c][:, n0:n0 + 2 * P, :].rearrange("p n (u e) -> p n u e", u=2),
                                     in0=xt[:].rearrange("p u i r -> p (u i r)").bitcast(BF16).rearrange("p (u n e) -> p n u e", u=2, e=2),
                                     in1=s_kp[:].rearrange("p (u e) -> p u e", u=2).unsqueeze(1).to_broadcast([P, 2 * P, 2, 2]), op=ALU.mult)
+
+        def widen_tile(i):
+            if C0[i] == "s":
+                nc.scalar.copy(out=xw[0][:, i, :], in_=xb[0][:, i, :].bitcast(FP8))
+            else:
+                nc.vector.tensor_scalar(out=xw[0][:, i, :].rearrange("p (u n e) -> p n u e", u=2, e=2),
+                                        in0=xb[0][:, i, :].bitcast(FP8).rearrange("p (n u e) -> p n u e", u=2, e=2),
+                                        scalar1=ones[:, 0:1], scalar2=None, op0=ALU.mult)
+
+        def turn_tile(i):
+            xt = psh.tile([P, CHUNK], F32, tag="h%d" % i, name="xt0")
+            for u in range(2):
+                wi = xw[0][:, i, :].bitcast(F32)
+                nc.tensor.transpose(xt[:, u * P:(u + 1) * P], wi[:, u:2 * P:2] if C0[i] == "s" else wi[:, u * P:(u + 1) * P], ident[:])
+            nc.vector.tensor_tensor(out=xg[0][:, i * P:(i + 1) * P, :].rearrange("p n (u e) -> p n u e", u=2),
+                                    in0=xt[:, 0:2 * P].bitcast(BF16).rearrange("p (u n e) -> p n u e", u=2, e=2),
+                                    in1=s_kp[:].rearrange("p (u e) -> p u e", u=2).unsqueeze(1).to_broadcast([P, P, 2, 2]), op=ALU.mult)
 
         def turn_w(pair):
             wt = pst.tile([P, 2, 2, P], F32, tag="t")
@@ -136,9 +162,11 @@ def tile_cvim_pa_kernel(tc, x_bytes, x_scale, w1, b1, w2, b2, out):
         def s_taps(c, m):
             b, c0 = c // 2, (c % 2) * CHUNK
             H = h_t[(c, m)][:]
-            if FORM[b][m] in "gG":
+            if FORM[b][m] in "gGx":
                 hr = hrow[(b, m)]
                 nc.scalar.activation(out=hr[:, c0:c0 + CHUNK], in_=H, func=ACT.Identity, bias=b1_f[:, m:m + 1])
+                if FORM[b][m] == "x":
+                    return
                 if FORM[b][m] == "G":
                     nc.scalar.activation(out=row1[:, b, m, 1 + c0:1 + c0 + CHUNK], in_=H, func=ACT.Identity, scale=a_f[:, m, 1:2], bias=k1[:, m:m + 1])
                 if FORM[b][m] in "gG":
@@ -148,19 +176,28 @@ def tile_cvim_pa_kernel(tc, x_bytes, x_scale, w1, b1, w2, b2, out):
                                             in1=a_f[:, m, 2:3].to_broadcast([P, CHUNK]), op=ALU.mult)
                 return
             nc.scalar.activation(out=row0[:, b, m, 1 + c0:1 + c0 + CHUNK], in_=H, func=ACT.Identity, scale=a_f[:, m, 0:1], bias=kall[:, m:m + 1])
-            if FORM[b][m] == "b":
+            if FORM[b][m] == "c":
+                nc.scalar.activation(out=row1[:, b, m, 1 + c0:1 + c0 + CHUNK], in_=H, func=ACT.Identity, scale=a_f[:, m, 1:2])
+            if FORM[b][m] in "bc":
                 nc.scalar.activation(out=row2[:, b, m, PADY - 1 + c0:PADY - 1 + c0 + CHUNK], in_=H, func=ACT.Identity, scale=a_f[:, m, 2:3])
 
         def vv(c, m, lo=0, hi=CHUNK):
             b, c0 = c // 2, (c % 2) * CHUNK
             H = h_t[(c, m)][:, lo:hi]
-            if FORM[b][m] == "G":
+            if FORM[b][m] in "cGx":
                 return
             if FORM[b][m] == "g":
                 nc.vector.tensor_scalar(out=row1[:, b, m, 1 + c0 + lo:1 + c0 + hi], in0=H, scalar1=a_f[:, m, 1:2], scalar2=k1[:, m:m + 1], op0=ALU.mult, op1=ALU.add)
             else:
                 nc.vector.scalar_tensor_tensor(out=row1[:, b, m, 1 + c0 + lo:1 + c0 + hi], in0=H, scalar=a_f[:, m, 1:2],
                                                in1=row0[:, b, m, c0 + lo:c0 + hi], op0=ALU.mult, op1=ALU.add)
+
+        def xx(m):
+            if FORM[0][m] == "x":
+                hr = hrow[(0, m)]
+                nc.vector.tensor_scalar(out=row0[:, 0, m, 1:1 + T], in0=hr[:], scalar1=a_f[:, m, 0:1], scalar2=None, op0=ALU.mult)
+                nc.vector.tensor_scalar(out=row1[:, 0, m, 1:1 + T], in0=hr[:], scalar1=a_f[:, m, 1:2], scalar2=b2_f[:, m:m + 1], op0=ALU.mult, op1=ALU.add)
+                nc.vector.tensor_scalar(out=row2[:, 0, m, PADY - 1:PADY - 1 + T], in0=hr[:], scalar1=a_f[:, m, 2:3], scalar2=None, op0=ALU.mult)
 
         def zz(c, m, lo=0, hi=CHUNK):
             b, c0 = c // 2, (c % 2) * CHUNK
@@ -180,7 +217,7 @@ def tile_cvim_pa_kernel(tc, x_bytes, x_scale, w1, b1, w2, b2, out):
                 parts = [row2[:, b, m, PADY + t0:PADY + t0 + P]]
                 if FORM[b][m] != "s":
                     parts = [row1[:, b, m, 1 + t0:1 + t0 + P]] + parts
-                if FORM[b][m] in "gG":
+                if FORM[b][m] in "cgG":
                     parts = [row0[:, b, m, t0:t0 + P]] + parts
                 for n, part in enumerate(parts):
                     nc.tensor.matmul(out=yT[:, m, :], lhsT=part, rhs=ident[:], is_transpose=True, start=n == 0, stop=n == len(parts) - 1)
@@ -213,34 +250,35 @@ def tile_cvim_pa_kernel(tc, x_bytes, x_scale, w1, b1, w2, b2, out):
                 for m in range(MT):
                     if FORM[b][m] == "s":
                         nc.vector.memset(row1[:, b, m, 0:1], 0.0)
-                    if FORM[b][m] in "gG":
+                    if FORM[b][m] in "gGx":
                         nc.vector.memset(row0[:, b, m, 0:1], 0.0)
                         nc.vector.memset(row2[:, b, m, PADY + T - 1:PADY + T], 0.0)
 
             a_f = const.tile([P, MT, 3], F32, name="a_f")
             ab = const.tile([P, MT, 3], F32, name="ab")
             b1_f = const.tile([P, MT], F32, name="b1_f")
+            b2_f = const.tile([P, MT], F32, name="b2_f")
             k1 = const.tile([P, MT], F32, name="k1")
             pad0 = const.tile([P, MT], F32, name="pad0")
             kall = const.tile([P, MT], F32, name="kall")
             na2b1 = const.tile([P, MT], F32, name="na2b1")
             nc.gpsimd.tensor_copy(out=a_f[:], in_=a_bf[:])
             nc.gpsimd.tensor_copy(out=b1_f[:], in_=b1_bf[:])
+            nc.gpsimd.tensor_copy(out=b2_f[:], in_=b2_bf[:])
             nc.gpsimd.tensor_tensor(out=ab[:], in0=a_f[:], in1=b1_f[:].unsqueeze(2).to_broadcast([P, MT, 3]), op=ALU.mult)
             nc.gpsimd.tensor_tensor(out=k1[:], in0=ab[:, :, 1], in1=b2_bf[:], op=ALU.add)
             nc.gpsimd.tensor_tensor(out=pad0[:], in0=ab[:, :, 2], in1=k1[:], op=ALU.add)
             nc.gpsimd.tensor_tensor(out=kall[:], in0=ab[:, :, 0], in1=pad0[:], op=ALU.add)
             for b in range(NB):
-                ms = [m for m in range(MT) if FORM[b][m] in "bs"]
-                nc.gpsimd.tensor_copy(out=row0[:, b, ms[0]:ms[-1] + 1, 0], in_=pad0[:, ms[0]:ms[-1] + 1])
+                ms = [m for m in range(MT) if FORM[b][m] in "bcs"]
+                if ms:
+                    nc.gpsimd.tensor_copy(out=row0[:, b, ms[0]:ms[-1] + 1, 0], in_=pad0[:, ms[0]:ms[-1] + 1])
 
-            widen(0, 0)
-            widen(0, 1)
+            for i in range(4):
+                widen_tile(i)
             widen(1, 0)
-            xt = turn_x(0, 0)
-            scale_x(0, 0, xt)
-            xt = turn_x(0, 1)
-            scale_x(0, 1, xt)
+            for i in range(4):
+                turn_tile(i)
             turn_w(0)
             turn_w(1)
             widen(1, 1)
@@ -260,8 +298,10 @@ def tile_cvim_pa_kernel(tc, x_bytes, x_scale, w1, b1, w2, b2, out):
             widen(3, 0)
             widen(3, 1)
             nc.gpsimd.tensor_scalar(out=na2b1[:], in0=ab[:, :, 2], scalar1=-1.0, scalar2=0.0, op0=ALU.mult, op1=ALU.add)
-            n = sum(f == "b" for f in FORM[0])
-            nc.gpsimd.tensor_copy(out=row2[:, 0, 0:n, PADY - 1 + T], in_=na2b1[:, 0:n])
+            for b in range(NB):
+                ms = [m for m in range(MT) if FORM[b][m] in "bc"]
+                if ms:
+                    nc.gpsimd.tensor_copy(out=row2[:, b, ms[0]:ms[-1] + 1, PADY - 1 + T], in_=na2b1[:, ms[0]:ms[-1] + 1])
             xt2 = [turn_x(2, 0), turn_x(2, 1)]
             quant(1)
         s_taps(0, 2)
@@ -289,6 +329,9 @@ def tile_cvim_pa_kernel(tc, x_bytes, x_scale, w1, b1, w2, b2, out):
                 for hf in range(2):
                     xt = xt2[hf] if c == 0 else turn_x(c + 2, hf)
                     scale_x(c + 2, hf, xt)
+            if c == XC:
+                for m in XM[0]:
+                    xx(m)
             vv(c, 2)
             zz(c, 1)
             mm(c + 1, 1)
@@ -302,5 +345,8 @@ def tile_cvim_pa_kernel(tc, x_bytes, x_scale, w1, b1, w2, b2, out):
             zz(c, 3)
             mm(c + 1, 3)
             s_taps(c + 1, 3)
+            if c == XC:
+                for m in XM[1]:
+                    xx(m)
             emit(DRAIN[c][3])
         emit(16 - nxt[0])

from contextlib import ExitStack

import concourse.masks as masks
import concourse.mybir as mybir

F32 = mybir.dt.float32
BF16 = mybir.dt.bfloat16
U32 = mybir.dt.uint32
U8 = mybir.dt.uint8
FP8 = mybir.dt.float8_e4m3fn
FP8X4 = mybir.dt.float8_e4m3fn_x4
ALU = mybir.AluOpType
ACT = mybir.ActivationFunctionType
ENG = mybir.EngineType

NB, T, C, D = 2, 1024, 512, 512
P = 128
CHUNK = 512
NCH = NB * T // CHUNK
MT = D // P
PADY = 16

FLOPS = 2 * NB * T * C * D + 6 * NB * T * D

CAST = ("pp", "ss", "sg", "gg")
FORM = ("bbbG", "ssss")
XC = 1
C0 = "ssss"
GSC = ()
XM = ((0, 1), (2, 3))
PIECES = ((0, 256), (256, 384), (384, 512))
EYPAT = "ssssssssssssssvs"
DRAIN = ((0, 0, 0, 0), (0, 0, 3, 0), (0, 3, 0, 2), (3, 0, 0, 0))


def tile_cvim_pa_kernel(tc, x_bytes, x_scale, w1, b1, w2, b2, out):
    nc = tc.nc
    xflat = x_bytes.rearrange("b t k -> (b t) k")
    oflat = out.rearrange("b t d -> (b t) d")

    with ExitStack() as ctx:
        const = ctx.enter_context(tc.tile_pool(name="const", bufs=1))
        rows = ctx.enter_context(tc.tile_pool(name="rows", bufs=1))
        outp = ctx.enter_context(tc.tile_pool(name="outp", bufs=16))
        psh = ctx.enter_context(tc.psum_pool(name="psh", bufs=1))
        pst = ctx.enter_context(tc.psum_pool(name="pst", bufs=4))

        a_bf = const.tile([P, MT, 3], BF16, name="a_bf")
        b1_bf = const.tile([P, MT], BF16, name="b1_bf")
        b2_bf = const.tile([P, MT], BF16, name="b2_bf")
        s_kp = const.tile([P, 4], F32, name="s_kp")
        w_sb = const.tile([P, MT, C], BF16, name="w_sb")
        wg = const.tile([P, D, 4], BF16, name="wg", align_bytes=64)
        wc = const.tile([P, D], U32, name="wc", align_bytes=64)
        ws = const.tile([P, D], U8, name="ws", align_bytes=64)
        ident = const.tile([P, P], F32, name="ident")
        ones = const.tile([P, 1], F32, name="ones")
        warm = const.tile([P, 2], F32, name="warm")
        xb, xw, xg, xc, xs, h_t, yT_t = [], [], [], [], [], {}, {}
        for c in range(NCH):
            xbt = const.tile([P, 4, C], U8, name="xbytes%d" % c)
            xwt = const.tile([P, 4, C], BF16, name="xw%d" % c)
            xgt = const.tile([P, CHUNK, 4], BF16, name="xg%d" % c, align_bytes=64)
            xct = const.tile([P, CHUNK], U32, name="xc%d" % c, align_bytes=64)
            xst = const.tile([P, CHUNK], U8, name="xs%d" % c, align_bytes=64)
            xb.append(xbt)
            xw.append(xwt)
            xg.append(xgt)
            xc.append(xct)
            xs.append(xst)
        row0 = rows.tile([P, NB, MT, 1 + T], F32, name="row0")
        row1 = rows.tile([P, NB, MT, 1 + T], F32, name="row1")
        row2 = rows.tile([P, NB, MT, PADY + T], F32, name="row2")
        hrow = {}
        for b in range(NB):
            for m in range(MT):
                if FORM[b][m] in "gGx":
                    hrow[(b, m)] = rows.tile([P, T], F32, name="h_%d_%d" % (b, m))

        for hf in range(2):
            nc.sync.dma_start(out=xb[0][:, 2 * hf:2 * hf + 2, :], in_=xflat[hf * 2 * P:(hf + 1) * 2 * P, :].rearrange("(i p) k -> p i k", p=P))
        nc.sync.dma_start(out=s_kp[:], in_=x_scale.rearrange("a b (p t) -> (a b p) t", t=4))
        nc.sync.dma_start(out=a_bf[:], in_=w2.rearrange("(p m) j -> p m j", m=MT))
        nc.sync.dma_start(out=b1_bf[:], in_=b1.rearrange("(p m) -> p m", m=MT))
        nc.sync.dma_start(out=b2_bf[:], in_=b2.rearrange("(p m) -> p m", m=MT))
        nc.sync.dma_start(out=w_sb[:], in_=w1.rearrange("(p m) k -> p m k", m=MT))
        for c in range(1, NCH):
            nc.sync.dma_start(out=xb[c][:], in_=xflat[c * CHUNK:(c + 1) * CHUNK, :].rearrange("(i p) k -> p i k", p=P))

        def widen(c, hf):
            dst = xw[c][:, 2 * hf:2 * hf + 2, :].rearrange("p i k -> p (i k)")
            src = xb[c][:, 2 * hf:2 * hf + 2, :].rearrange("p i k -> p (i k)").bitcast(FP8)
            if CAST[c][hf] == "p":
                nc.vector.tensor_scalar(out=dst.rearrange("p (u n e) -> p n u e", u=2, e=2), in0=src.rearrange("p (n u e) -> p n u e", u=2, e=2),
                                        scalar1=ones[:, 0:1], scalar2=None, op0=ALU.mult)
            elif CAST[c][hf] == "s":
                nc.scalar.copy(out=dst, in_=src)
            else:
                nc.gpsimd.tensor_copy(out=dst, in_=src)

        def words(src, pair):
            return src[:, 2 * pair:2 * pair + 2, :].rearrange("p i k -> p (i k)").bitcast(F32)

        def turn_x(c, hf):
            xt = pst.tile([P, 2, 2, P], F32, tag="t")
            for i2 in range(2):
                for u in range(2):
                    lo = (2 * u + i2) * P if CAST[c][hf] == "p" else 2 * i2 * P + u
                    step = 1 if CAST[c][hf] == "p" else 2
                    nc.tensor.transpose(xt[:, i2, u, :] if (c, hf) in GSC else xt[:, u, i2, :], words(xw[c], hf)[:, lo:lo + (P - 1) * step + 1:step], ident[:])
            return xt

        def scale_x(c, hf, xt):
            n0 = 2 * hf * P
            if (c, hf) in GSC:
                raw = const.tile([P, 2 * P, 4], BF16, name="raw%d%d" % (c, hf))
                nc.scalar.copy(out=raw[:].rearrange("p n j -> p (n j)").bitcast(F32).rearrange("p (i r u) -> p i r u", i=2, u=2), in_=xt[:].rearrange("p i u r -> p i r u"))
                nc.gpsimd.tensor_tensor(out=xg[c][:, n0:n0 + 2 * P, :], in0=raw[:], in1=s_kp[:].unsqueeze(1).to_broadcast([P, 2 * P, 4]), op=ALU.mult)
                return
            nc.vector.tensor_tensor(out=xg[c][:, n0:n0 + 2 * P, :].rearrange("p n (u e) -> p n u e", u=2),
                                    in0=xt[:].rearrange("p u i r -> p (u i r)").bitcast(BF16).rearrange("p (u n e) -> p n u e", u=2, e=2),
                                    in1=s_kp[:].rearrange("p (u e) -> p u e", u=2).unsqueeze(1).to_broadcast([P, 2 * P, 2, 2]), op=ALU.mult)

        def widen_tile(i):
            if C0[i] == "s":
                nc.scalar.copy(out=xw[0][:, i, :], in_=xb[0][:, i, :].bitcast(FP8))
            else:
                nc.vector.tensor_scalar(out=xw[0][:, i, :].rearrange("p (u n e) -> p n u e", u=2, e=2),
                                        in0=xb[0][:, i, :].bitcast(FP8).rearrange("p (n u e) -> p n u e", u=2, e=2),
                                        scalar1=ones[:, 0:1], scalar2=None, op0=ALU.mult)

        def turn_tile(i):
            xt = psh.tile([P, CHUNK], F32, tag="h%d" % i, name="xt0")
            for u in range(2):
                wi = xw[0][:, i, :].bitcast(F32)
                nc.tensor.transpose(xt[:, u * P:(u + 1) * P], wi[:, u:2 * P:2] if C0[i] == "s" else wi[:, u * P:(u + 1) * P], ident[:])
            nc.vector.tensor_tensor(out=xg[0][:, i * P:(i + 1) * P, :].rearrange("p n (u e) -> p n u e", u=2),
                                    in0=xt[:, 0:2 * P].bitcast(BF16).rearrange("p (u n e) -> p n u e", u=2, e=2),
                                    in1=s_kp[:].rearrange("p (u e) -> p u e", u=2).unsqueeze(1).to_broadcast([P, P, 2, 2]), op=ALU.mult)

        def turn_w(pair):
            wt = pst.tile([P, 2, 2, P], F32, tag="t")
            for i2 in range(2):
                for u in range(2):
                    lo = 2 * i2 * P + u
                    nc.tensor.transpose(wt[:, i2, u, :], words(w_sb, pair)[:, lo:lo + 2 * P - 1:2], ident[:])
            dst = wg[:, 2 * pair * P:(2 * pair + 2) * P, :].rearrange("p n j -> p (n j)").bitcast(F32)
            nc.scalar.copy(out=dst.rearrange("p (i r u) -> p i r u", i=2, u=2), in_=wt[:].rearrange("p i u r -> p i r u"))

        def quant_w():
            nc.vector.quantize_mx(out=wc[:].bitcast(FP8X4), scales=ws[:], in_=wg[:].rearrange("p n j -> p (n j)"))

        def quant(c):
            nc.vector.quantize_mx(out=xc[c][:].bitcast(FP8X4), scales=xs[c][:], in_=xg[c][:].rearrange("p n j -> p (n j)"))

        def mm(c, m):
            h = psh.tile([P, CHUNK], F32, tag="h%d" % m)
            h_t[(c, m)] = h
            nc.tensor.matmul_mx(out=h[:], lhsT=wc[:, m * P:(m + 1) * P].bitcast(FP8X4), lhsT_scale=ws[:, m * P:(m + 1) * P],
                                rhs=xc[c][:].bitcast(FP8X4), rhs_scale=xs[c][:], start=True, stop=True)

        def s_taps(c, m):
            b, c0 = c // 2, (c % 2) * CHUNK
            H = h_t[(c, m)][:]
            if FORM[b][m] in "gGx":
                hr = hrow[(b, m)]
                nc.scalar.activation(out=hr[:, c0:c0 + CHUNK], in_=H, func=ACT.Identity, bias=b1_f[:, m:m + 1])
                if FORM[b][m] == "x":
                    return
                if FORM[b][m] == "G":
                    nc.scalar.activation(out=row1[:, b, m, 1 + c0:1 + c0 + CHUNK], in_=H, func=ACT.Identity, scale=a_f[:, m, 1:2], bias=k1[:, m:m + 1])
                if FORM[b][m] in "gG":
                    nc.gpsimd.tensor_tensor(out=row0[:, b, m, 1 + c0:1 + c0 + CHUNK], in0=hr[:, c0:c0 + CHUNK],
                                            in1=a_f[:, m, 0:1].to_broadcast([P, CHUNK]), op=ALU.mult)
                    nc.gpsimd.tensor_tensor(out=row2[:, b, m, PADY - 1 + c0:PADY - 1 + c0 + CHUNK], in0=hr[:, c0:c0 + CHUNK],
                                            in1=a_f[:, m, 2:3].to_broadcast([P, CHUNK]), op=ALU.mult)
                return
            nc.scalar.activation(out=row0[:, b, m, 1 + c0:1 + c0 + CHUNK], in_=H, func=ACT.Identity, scale=a_f[:, m, 0:1], bias=kall[:, m:m + 1])
            if FORM[b][m] == "c":
                nc.scalar.activation(out=row1[:, b, m, 1 + c0:1 + c0 + CHUNK], in_=H, func=ACT.Identity, scale=a_f[:, m, 1:2])
            if FORM[b][m] in "bc":
                nc.scalar.activation(out=row2[:, b, m, PADY - 1 + c0:PADY - 1 + c0 + CHUNK], in_=H, func=ACT.Identity, scale=a_f[:, m, 2:3])

        def vv(c, m, lo=0, hi=CHUNK):
            b, c0 = c // 2, (c % 2) * CHUNK
            H = h_t[(c, m)][:, lo:hi]
            if FORM[b][m] in "cGx":
                return
            if FORM[b][m] == "g":
                nc.vector.tensor_scalar(out=row1[:, b, m, 1 + c0 + lo:1 + c0 + hi], in0=H, scalar1=a_f[:, m, 1:2], scalar2=k1[:, m:m + 1], op0=ALU.mult, op1=ALU.add)
            else:
                nc.vector.scalar_tensor_tensor(out=row1[:, b, m, 1 + c0 + lo:1 + c0 + hi], in0=H, scalar=a_f[:, m, 1:2],
                                               in1=row0[:, b, m, c0 + lo:c0 + hi], op0=ALU.mult, op1=ALU.add)

        def xx(m):
            if FORM[0][m] == "x":
                hr = hrow[(0, m)]
                nc.vector.tensor_scalar(out=row0[:, 0, m, 1:1 + T], in0=hr[:], scalar1=a_f[:, m, 0:1], scalar2=None, op0=ALU.mult)
                nc.vector.tensor_scalar(out=row1[:, 0, m, 1:1 + T], in0=hr[:], scalar1=a_f[:, m, 1:2], scalar2=b2_f[:, m:m + 1], op0=ALU.mult, op1=ALU.add)
                nc.vector.tensor_scalar(out=row2[:, 0, m, PADY - 1:PADY - 1 + T], in0=hr[:], scalar1=a_f[:, m, 2:3], scalar2=None, op0=ALU.mult)

        def zz(c, m, lo=0, hi=CHUNK):
            b, c0 = c // 2, (c % 2) * CHUNK
            if FORM[b][m] != "s":
                return
            nc.vector.scalar_tensor_tensor(out=row2[:, b, m, PADY - 1 + c0 + lo:PADY - 1 + c0 + hi], in0=h_t[(c, m)][:, lo:hi], scalar=a_f[:, m, 2:3],
                                           in1=row1[:, b, m, c0 + lo:c0 + hi], op0=ALU.mult, op1=ALU.add)
            if c0 + hi == T:
                nc.vector.tensor_scalar(out=row2[:, b, m, PADY + T - 1:PADY + T], in0=row1[:, b, m, T:T + 1],
                                        scalar1=na2b1[:, m:m + 1], scalar2=None, op0=ALU.add)

        def ty(b, i):
            t0 = i * P
            yT = pst.tile([P, MT, P], F32, tag="t", name="yT")
            yT_t[(b, i)] = yT
            for m in range(MT):
                parts = [row2[:, b, m, PADY + t0:PADY + t0 + P]]
                if FORM[b][m] != "s":
                    parts = [row1[:, b, m, 1 + t0:1 + t0 + P]] + parts
                if FORM[b][m] in "cgG":
                    parts = [row0[:, b, m, t0:t0 + P]] + parts
                for n, part in enumerate(parts):
                    nc.tensor.matmul(out=yT[:, m, :], lhsT=part, rhs=ident[:], is_transpose=True, start=n == 0, stop=n == len(parts) - 1)

        def ey(b, i, eng):
            t0 = i * P
            ysb = outp.tile([P, D], F32, tag="ysb")
            dst, src = ysb[:].rearrange("p (q m) -> p q m", m=MT), yT_t[(b, i)][:].rearrange("p m q -> p q m")
            if eng == "s":
                nc.scalar.copy(out=dst, in_=src)
            else:
                nc.vector.tensor_copy(out=dst, in_=src)
            nc.sync.dma_start(out=oflat[b * T + t0:b * T + t0 + P, :], in_=ysb[:])

        nxt = [0]

        def emit(n):
            for j in range(n):
                b, i = nxt[0] // 8, nxt[0] % 8
                ty(b, i)
                ey(b, i, EYPAT[nxt[0]])
                nxt[0] += 1

        with tc.manual_schedule(engines={ENG.Pool, ENG.DVE, ENG.PE, ENG.Activation}):
            masks.make_identity(nc, ident[:])
            nc.vector.memset(ones[:], 1.0)
            nc.vector.memset(warm[:, 0:1], 0.0)
            nc.scalar.activation(out=warm[:, 1:2], in_=warm[:, 0:1], func=ACT.Identity)
            for b in range(NB):
                for m in range(MT):
                    if FORM[b][m] == "s":
                        nc.vector.memset(row1[:, b, m, 0:1], 0.0)
                    if FORM[b][m] in "gGx":
                        nc.vector.memset(row0[:, b, m, 0:1], 0.0)
                        nc.vector.memset(row2[:, b, m, PADY + T - 1:PADY + T], 0.0)

            a_f = const.tile([P, MT, 3], F32, name="a_f")
            ab = const.tile([P, MT, 3], F32, name="ab")
            b1_f = const.tile([P, MT], F32, name="b1_f")
            b2_f = const.tile([P, MT], F32, name="b2_f")
            k1 = const.tile([P, MT], F32, name="k1")
            pad0 = const.tile([P, MT], F32, name="pad0")
            kall = const.tile([P, MT], F32, name="kall")
            na2b1 = const.tile([P, MT], F32, name="na2b1")
            nc.gpsimd.tensor_copy(out=a_f[:], in_=a_bf[:])
            nc.gpsimd.tensor_copy(out=b1_f[:], in_=b1_bf[:])
            nc.gpsimd.tensor_copy(out=b2_f[:], in_=b2_bf[:])
            nc.gpsimd.tensor_tensor(out=ab[:], in0=a_f[:], in1=b1_f[:].unsqueeze(2).to_broadcast([P, MT, 3]), op=ALU.mult)
            nc.gpsimd.tensor_tensor(out=k1[:], in0=ab[:, :, 1], in1=b2_bf[:], op=ALU.add)
            nc.gpsimd.tensor_tensor(out=pad0[:], in0=ab[:, :, 2], in1=k1[:], op=ALU.add)
            nc.gpsimd.tensor_tensor(out=kall[:], in0=ab[:, :, 0], in1=pad0[:], op=ALU.add)
            for b in range(NB):
                ms = [m for m in range(MT) if FORM[b][m] in "bcs"]
                if ms:
                    nc.gpsimd.tensor_copy(out=row0[:, b, ms[0]:ms[-1] + 1, 0], in_=pad0[:, ms[0]:ms[-1] + 1])

            for i in range(4):
                widen_tile(i)
            widen(1, 0)
            for i in range(4):
                turn_tile(i)
            turn_w(0)
            turn_w(1)
            widen(1, 1)
            widen(2, 0)
            quant(0)
            quant_w()
            for hf in range(2):
                xt = turn_x(1, hf)
                scale_x(1, hf, xt)
            mm(0, 0)
            s_taps(0, 0)
            mm(0, 1)
            s_taps(0, 1)
            mm(0, 2)
            mm(0, 3)
            widen(2, 1)
            widen(3, 0)
            widen(3, 1)
            nc.gpsimd.tensor_scalar(out=na2b1[:], in0=ab[:, :, 2], scalar1=-1.0, scalar2=0.0, op0=ALU.mult, op1=ALU.add)
            for b in range(NB):
                ms = [m for m in range(MT) if FORM[b][m] in "bc"]
                if ms:
                    nc.gpsimd.tensor_copy(out=row2[:, b, ms[0]:ms[-1] + 1, PADY - 1 + T], in_=na2b1[:, ms[0]:ms[-1] + 1])
            xt2 = [turn_x(2, 0), turn_x(2, 1)]
            quant(1)
        s_taps(0, 2)
        s_taps(0, 3)
        for c in range(NCH):
            more = c + 1 < NCH
            if not more:
                emit(DRAIN[c][0])
                for lo, hi in PIECES:
                    for m in range(MT):
                        vv(c, m, lo, hi)
                    for m in range(MT):
                        zz(c, m, lo, hi)
                    emit(8 + (CHUNK + hi - 1) // P - nxt[0] if hi < CHUNK else 0)
                continue
            vv(c, 0)
            vv(c, 1)
            zz(c, 0)
            emit(DRAIN[c][0])
            if c > 0:
                quant(c + 1)
            mm(c + 1, 0)
            s_taps(c + 1, 0)
            if c + 2 < NCH:
                for hf in range(2):
                    xt = xt2[hf] if c == 0 else turn_x(c + 2, hf)
                    scale_x(c + 2, hf, xt)
            if c == XC:
                for m in XM[0]:
                    xx(m)
            vv(c, 2)
            zz(c, 1)
            mm(c + 1, 1)
            s_taps(c + 1, 1)
            emit(DRAIN[c][1])
            vv(c, 3)
            zz(c, 2)
            mm(c + 1, 2)
            s_taps(c + 1, 2)
            emit(DRAIN[c][2])
            zz(c, 3)
            mm(c + 1, 3)
            s_taps(c + 1, 3)
            if c == XC:
                for m in XM[1]:
                    xx(m)
            emit(DRAIN[c][3])
        emit(16 - nxt[0])
